import numpy as np
import ml_dtypes


def mxq(x, axis, fmt="e4m3"):
    dtype, down = {"e4m3": (ml_dtypes.float8_e4m3fn, 7), "e5m2": (ml_dtypes.float8_e5m2, 14)}[fmt]
    v = np.moveaxis(np.asarray(x, np.float32).astype(ml_dtypes.bfloat16).astype(np.float64), axis, -1)
    blocks = v.reshape(v.shape[:-1] + (-1, 32))
    amax = np.abs(blocks).max(-1, keepdims=True)
    byte = np.maximum(np.where(amax > 0, np.frexp(amax)[1] - 1 + 127, 0) - down, 1)
    scale = np.exp2(byte - 127.0)
    codes = (blocks / scale).astype(np.float32).astype(dtype).astype(np.float64)
    return np.moveaxis((codes * scale).reshape(v.shape), -1, axis)


WIDE = False


def mx_kscale(k):
    if not WIDE:
        return np.ones(k)
    levels = np.array([10, -10, 5, -5, 0])
    a = np.random.permutation(np.resize(levels, k // 512 * 4)).reshape(k // 512, 4)
    idx = np.arange(k)
    return np.exp2(a[idx // 512, idx % 128 // 32])


BF16 = ml_dtypes.bfloat16


def bf(x):
    return np.asarray(x, np.float32).astype(BF16)


def f64(x):
    return np.asarray(x).astype(np.float64)


M, DI, N, DO, TS = 256, 1024, 2048, 1024, 3
DENSITY = 0.25


def setup_inputs():
    k = mx_kscale(N)
    m = (np.random.uniform(size=(N, N)) < DENSITY).astype(np.float64)
    return {'state': bf(np.tanh(1.5 * np.random.standard_normal((M, N))) * k),
            'weights': bf(np.random.standard_normal((N, N)) * 1.5 / np.sqrt(DENSITY * N) / k[:, None]),
            'J': bf(np.random.standard_normal((N, N)) * 2.0 / np.sqrt(DENSITY * N)),
            'theta': bf(np.random.uniform(size=N) * 1.0 + 0.25),
            'lam': bf(0.35 + 0.05 * np.random.standard_normal(1)),
            'mask': bf(m * (1.0 - np.eye(N))),
            'noise_raw': bf(np.random.standard_normal((M, N)) * 2.5)}


def reference(state, weights, J, theta, lam, mask, noise_raw):
    st = f64(state)
    eff_w = f64(weights) * f64(mask)
    J_m = f64(J) * f64(mask)
    T = np.abs(np.sin(2.0 * f64(theta)))
    signal = mxq(st, 1, 'e4m3') @ mxq(eff_w, 0, 'e4m3')
    s = np.tanh(st)
    delta = (mxq(s, 1, 'e4m3') @ mxq(J_m, 0, 'e4m3')) * s
    noise = f64(noise_raw) * T * 0.1
    return np.tanh(signal + f64(lam) * delta + noise)

@@ -1,0 +1,233 @@
+import math
+from contextlib import ExitStack
+
+import concourse.mybir as mybir
+from concourse.masks import make_identity
+
+FP8X4 = mybir.dt.float8_e4m3fn_x4
+BF16 = mybir.dt.bfloat16
+F32 = mybir.dt.float32
+I32 = mybir.dt.int32
+U32 = mybir.dt.uint32
+U8 = mybir.dt.uint8
+ALU = mybir.AluOpType
+ACT = mybir.ActivationFunctionType
+
+P = 128
+M_ROWS = 256
+N = 2048
+M_TILES = 2
+PASSES = 4
+HALF = 1024
+UNIT = 512
+
+FLOPS = 2 * 2 * M_ROWS * N * N
+
+PI_HI = 3.140625
+PI_LO = math.pi - PI_HI
+SIN_COEF = (1.0, -1.0 / 6.0, 1.0 / 120.0, -1.0 / 5040.0, 1.0 / 362880.0, -1.0 / 39916800.0, 1.0 / 6227020800.0, -1.0 / 1307674368000.0)
+
+VECTOR_REGROUPS = (30, 31)
+PROD_BUFS = 6
+GRP_BUFS = 4
+CODE_BUFS = 10
+RAW_BUFS = 3
+
+
+def tile_brainquantumlayer_pb_kernel(tc, state, weights, J, theta, lam, mask, noise_raw, out):
+    nc = tc.nc
+    with ExitStack() as ctx:
+        const = ctx.enter_context(tc.tile_pool(name="const", bufs=1))
+        rawp = ctx.enter_context(tc.tile_pool(name="raw", bufs=RAW_BUFS))
+        prodp = ctx.enter_context(tc.tile_pool(name="prod", bufs=PROD_BUFS))
+        grpp = ctx.enter_context(tc.tile_pool(name="grp", bufs=GRP_BUFS))
+        codep = ctx.enter_context(tc.tile_pool(name="code", bufs=CODE_BUFS))
+        tmpp = ctx.enter_context(tc.tile_pool(name="tmp", bufs=2))
+        psum = ctx.enter_context(tc.psum_pool(name="psum", bufs=1))
+
+        ident = const.tile([P, P], F32, name="ident")
+        make_identity(nc, ident[:])
+        th_bf = const.tile([P, 16], BF16, name="th_bf")
+        nc.scalar.dma_start(
+            out=th_bf[:].rearrange("p (b i) -> p b i", i=4),
+            in_=theta.rearrange("(b p i) -> p b i", b=4, i=4),
+        )
+        lam_bf = const.tile([P, 1], BF16, name="lam_bf")
+        nc.scalar.dma_start(out=lam_bf[:], in_=lam.partition_broadcast(P))
+
+        st_sb = []
+        for mt in range(M_TILES):
+            t = const.tile([P, N], BF16, name="st%d" % mt)
+            nc.sync.dma_start(out=t[:], in_=state[mt * P:(mt + 1) * P, :])
+            st_sb.append(t)
+
+        def load_group(g):
+            h, c = divmod(g, PASSES)
+            rows = slice(c * 512, (c + 1) * 512)
+            cols = slice(h * HALF, (h + 1) * HALF)
+            tiles = []
+            for tag, src in (("J", J), ("K", mask), ("W", weights)):
+                t = rawp.tile([P, 4, HALF], BF16, tag=tag, name="raw%s%d" % (tag, g))
+                nc.sync.dma_start(out=t[:], in_=src[rows, cols].rearrange("(p j) w -> p j w", j=4))
+                tiles.append(t)
+            return tiles
+
+        groups = {}
+        groups[0] = load_group(0)
+        groups[1] = load_group(1)
+
+        noise_sb = []
+        for mt in range(M_TILES):
+            t = const.tile([P, N], BF16, name="noise%d" % mt)
+            nc.sync.dma_start(out=t[:], in_=noise_raw[mt * P:(mt + 1) * P, :])
+            noise_sb.append(t)
+
+        def small(name, dt=F32):
+            return const.tile([P, 16], dt, name=name)
+
+        lam32 = const.tile([P, 1], F32, name="lam32")
+        nc.vector.tensor_copy(out=lam32[:], in_=lam_bf[:])
+        k_i = small("k_i", I32)
+        nc.vector.tensor_scalar(out=k_i[:], in0=th_bf[:], scalar1=2.0 / math.pi, scalar2=None, op0=ALU.mult)
+        k_f = small("k_f")
+        nc.vector.tensor_copy(out=k_f[:], in_=k_i[:])
+        x2 = small("x2")
+        nc.vector.tensor_scalar(out=x2[:], in0=th_bf[:], scalar1=2.0, scalar2=None, op0=ALU.mult)
+        r1 = small("r1")
+        nc.vector.scalar_tensor_tensor(out=r1[:], in0=k_f[:], scalar=-PI_HI, in1=x2[:], op0=ALU.mult, op1=ALU.add)
+        r2 = small("r2")
+        nc.vector.scalar_tensor_tensor(out=r2[:], in0=k_f[:], scalar=-PI_LO, in1=r1[:], op0=ALU.mult, op1=ALU.add)
+        a_abs = small("a_abs")
+        nc.vector.scalar_tensor_tensor(out=a_abs[:], in0=r2[:], scalar=-1.0, in1=r2[:], op0=ALU.mult, op1=ALU.max)
+        a_ref = small("a_ref")
+        nc.vector.tensor_scalar(out=a_ref[:], in0=a_abs[:], scalar1=-1.0, scalar2=math.pi, op0=ALU.mult, op1=ALU.add)
+        a_min = small("a_min")
+        nc.vector.tensor_tensor(out=a_min[:], in0=a_abs[:], in1=a_ref[:], op=ALU.min)
+        z = small("z")
+        nc.vector.tensor_tensor(out=z[:], in0=a_min[:], in1=a_min[:], op=ALU.mult)
+        a01 = small("a01")
+        nc.vector.tensor_scalar(out=a01[:], in0=a_min[:], scalar1=0.1, scalar2=None, op0=ALU.mult)
+        w = small("w7")
+        nc.vector.tensor_scalar(out=w[:], in0=z[:], scalar1=SIN_COEF[7], scalar2=None, op0=ALU.mult)
+        for k in range(6, 0, -1):
+            w_next = small("w%d" % k)
+            nc.vector.scalar_tensor_tensor(out=w_next[:], in0=w[:], scalar=SIN_COEF[k], in1=z[:], op0=ALU.add, op1=ALU.mult)
+            w = w_next
+        tq = small("tq")
+        nc.vector.scalar_tensor_tensor(out=tq[:], in0=w[:], scalar=1.0, in1=a01[:], op0=ALU.add, op1=ALU.mult)
+
+        s32 = []
+        for mt in range(M_TILES):
+            t = const.tile([P, N], F32, name="s32_%d" % mt)
+            for q in range(2):
+                sl = slice(q * HALF, (q + 1) * HALF)
+                nc.scalar.activation(out=t[:, sl], in_=st_sb[mt][:, sl], func=ACT.Tanh)
+            s32.append(t)
+
+        st_codes = const.tile([P, PASSES * M_ROWS], U32, name="st_codes", align_bytes=64)
+        st_scales = const.tile([P, PASSES * M_ROWS], U8, name="st_scales", align_bytes=64)
+        s_codes = const.tile([P, PASSES * M_ROWS], U32, name="s_codes", align_bytes=64)
+        s_scales = const.tile([P, PASSES * M_ROWS], U8, name="s_scales", align_bytes=64)
+
+        words = [st_sb[mt][:].bitcast(F32).rearrange("m (c v u) -> m c u v", c=PASSES, u=2) for mt in range(M_TILES)]
+        xts = []
+        for c in range(PASSES):
+            xt = psum.tile([P, 512], F32, tag="bank%d" % c, name="xt%d" % c)
+            xt3 = xt[:].rearrange("p (u m) -> p u m", u=2)
+            for mt in range(M_TILES):
+                for u in range(2):
+                    nc.tensor.transpose(out=xt3[:, u, mt * P:(mt + 1) * P], in_=words[mt][:, c, u, :], identity=ident[:])
+            xts.append(xt)
+        for c in range(PASSES):
+            xt = xts[c]
+            cs = slice(c * M_ROWS, (c + 1) * M_ROWS)
+            g_s = grpp.tile([P, 1024], BF16, tag="grp", name="g_s%d" % c, align_bytes=64)
+            nc.scalar.activation(
+                out=g_s[:].rearrange("p (m u e) -> p m u e", u=2, e=2),
+                in_=xt[:].bitcast(BF16).rearrange("p (u m e) -> p m u e", u=2, e=2),
+                func=ACT.Tanh,
+            )
+            g_st = grpp.tile([P, 1024], BF16, tag="grp", name="g_st%d" % c, align_bytes=64)
+            nc.vector.tensor_copy(
+                out=g_st[:].bitcast(F32).rearrange("p (m u) -> p m u", u=2),
+                in_=xt[:].rearrange("p (u m) -> p m u", u=2),
+            )
+            nc.vector.quantize_mx(out=s_codes[:, cs].bitcast(FP8X4), scales=s_scales[:, cs], in_=g_s[:])
+            nc.vector.quantize_mx(out=st_codes[:, cs].bitcast(FP8X4), scales=st_scales[:, cs], in_=g_st[:])
+
+        acc = {}
+        for b in range(4):
+            tb = psum.tile([P, 512], F32, tag="bank%d" % (4 + b), name="tb%d" % b)
+            for i in range(4):
+                nc.tensor.matmul(
+                    out=tb[:, i * P:(i + 1) * P],
+                    lhsT=tq[:, 4 * b + i:4 * b + i + 1].to_broadcast([P, P]),
+                    rhs=ident[:],
+                    start=True,
+                    stop=True,
+                )
+            for mt in range(M_TILES):
+                a = const.tile([P, UNIT], F32, name="acc%d%d" % (mt, b))
+                nc.vector.tensor_tensor(
+                    out=a[:].rearrange("q (p i) -> q p i", i=4),
+                    in0=noise_sb[mt][:, b * UNIT:(b + 1) * UNIT].rearrange("q (p i) -> q p i", i=4),
+                    in1=tb[:].rearrange("q (i p) -> q p i", i=4),
+                    op=ALU.mult,
+                )
+                acc[(mt, b)] = a
+
+        unit_no = 0
+        banks = {}
+        for g in range(2 * PASSES):
+            h, c = divmod(g, PASSES)
+            if g + 2 < 2 * PASSES and g + 2 not in groups:
+                groups[g + 2] = load_group(g + 2)
+            jr, kr, wr = groups[g]
+            for mat, raw in ((0, jr), (1, wr)):
+                a_codes, a_scales = (s_codes, s_scales) if mat == 0 else (st_codes, st_scales)
+                for ntp in range(2):
+                    sl = slice(ntp * UNIT, (ntp + 1) * UNIT)
+                    nt = 2 * h + ntp
+                    prod = prodp.tile([P, 4, UNIT], BF16, tag="prod", name="prod%d" % unit_no)
+                    nc.vector.tensor_tensor(out=prod[:], in0=raw[:, :, sl], in1=kr[:, :, sl], op=ALU.mult)
+                    grp = grpp.tile([P, 4 * UNIT], BF16, tag="grp", name="grp%d" % unit_no, align_bytes=64)
+                    dst = grp[:].rearrange("p (c i t) -> p c t i", i=4, t=4)
+                    src = prod[:].rearrange("p t (c i) -> p c t i", i=4)
+                    if unit_no in VECTOR_REGROUPS:
+                        nc.vector.tensor_copy(out=dst, in_=src)
+                    else:
+                        nc.scalar.copy(out=dst, in_=src)
+                    codes = codep.tile([P, UNIT], U32, tag="codes", name="codes%d" % unit_no, align_bytes=64)
+                    scl = codep.tile([P, UNIT], U8, tag="scl", name="scl%d" % unit_no, align_bytes=64)
+                    nc.vector.quantize_mx(out=codes[:].bitcast(FP8X4), scales=scl[:], in_=grp[:])
+                    for mt in range(M_TILES):
+                        idx = mat * 4 + mt * 2 + ntp
+                        if c == 0:
+                            banks[idx] = psum.tile([P, UNIT], F32, tag="bank%d" % idx, name="acc_ps%d_%d" % (h, idx))
+                        ms = slice(c * M_ROWS + mt * P, c * M_ROWS + (mt + 1) * P)
+                        nc.tensor.matmul_mx(
+                            out=banks[idx][:],
+                            lhsT=a_codes[:, ms].bitcast(FP8X4),
+                            lhsT_scale=a_scales[:, ms],
+                            rhs=codes[:].bitcast(FP8X4),
+                            rhs_scale=scl[:],
+                            start=(c == 0),
+                            stop=(c == PASSES - 1),
+                        )
+                    if c == PASSES - 1:
+                        ns = slice(nt * UNIT, (nt + 1) * UNIT)
+                        for mt in range(M_TILES):
+                            idx = mat * 4 + mt * 2 + ntp
+                            a = acc[(mt, nt)]
+                            if mat == 0:
+                                tmp = tmpp.tile([P, UNIT], F32, tag="tmp", name="tmp%d%d" % (mt, nt))
+                                nc.vector.scalar_tensor_tensor(
+                                    out=tmp[:], in0=banks[idx][:], scalar=lam32[:, 0:1], in1=s32[mt][:, ns],
+                                    op0=ALU.mult, op1=ALU.mult,
+                                )
+                                nc.vector.tensor_tensor(out=a[:], in0=tmp[:], in1=a[:], op=ALU.add)
+                            else:
+                                nc.vector.tensor_tensor(out=a[:], in0=banks[idx][:], in1=a[:], op=ALU.add)
+                                nc.scalar.activation(out=a[:], in_=a[:], func=ACT.Tanh)
+                                nc.sync.dma_start(out=out[mt * P:(mt + 1) * P, ns], in_=a[:])
+                    unit_no += 1

@@ -27,11 +27,25 @@ PI_HI = 3.140625
 PI_LO = math.pi - PI_HI
 SIN_COEF = (1.0, -1.0 / 6.0, 1.0 / 120.0, -1.0 / 5040.0, 1.0 / 362880.0, -1.0 / 39916800.0, 1.0 / 6227020800.0, -1.0 / 1307674368000.0)
 
-VECTOR_REGROUPS = (30, 31)
+VECTOR_REGROUPS = (0, 1, 2, 3)
 PROD_BUFS = 6
-GRP_BUFS = 4
+GRP_BUFS = 5
 CODE_BUFS = 10
 RAW_BUFS = 3
+UNITS = 32
+CHAIN_FIRST = 12
+
+
+def lead(i):
+    return 1 if i < 3 else (2 if i < 7 else 4)
+
+
+def lag_vec(i):
+    return 5 if i < 28 else 2
+
+
+def lag_act(i):
+    return 8 if i < 28 else 3
 
 
 def tile_brainquantumlayer_pb_kernel(tc, state, weights, J, theta, lam, mask, noise_raw, out):
@@ -44,6 +58,13 @@ def tile_brainquantumlayer_pb_kernel(tc, state, weights, J, theta, lam, mask, no
         codep = ctx.enter_context(tc.tile_pool(name="code", bufs=CODE_BUFS))
         tmpp = ctx.enter_context(tc.tile_pool(name="tmp", bufs=2))
         psum = ctx.enter_context(tc.psum_pool(name="psum", bufs=1))
+        ctx.enter_context(tc.manual_schedule())
+
+        units = []
+        for g in range(2 * PASSES):
+            order = ((0, 0), (1, 0), (0, 1), (1, 1)) if g == 0 else ((0, 0), (0, 1), (1, 0), (1, 1))
+            for mat, ntp in order:
+                units.append((g, mat, ntp))
 
         ident = const.tile([P, P], F32, name="ident")
         make_identity(nc, ident[:])
@@ -55,66 +76,106 @@ def tile_brainquantumlayer_pb_kernel(tc, state, weights, J, theta, lam, mask, no
         lam_bf = const.tile([P, 1], BF16, name="lam_bf")
         nc.scalar.dma_start(out=lam_bf[:], in_=lam.partition_broadcast(P))
 
-        st_sb = []
-        for mt in range(M_TILES):
-            t = const.tile([P, N], BF16, name="st%d" % mt)
-            nc.sync.dma_start(out=t[:], in_=state[mt * P:(mt + 1) * P, :])
-            st_sb.append(t)
+        sources = {"J": J, "K": mask, "W": weights}
+        groups = {}
+
+        def alloc_group(g):
+            groups[g] = {}
+            for tag in ("J", "K", "W"):
+                groups[g][tag] = rawp.tile([P, 4, HALF], BF16, tag=tag, name="raw%s%d" % (tag, g))
+
+        def load_piece(g, tag, lo, hi):
+            h, c = divmod(g, PASSES)
+            src = sources[tag][c * 512:(c + 1) * 512, h * HALF + lo:h * HALF + hi]
+            nc.sync.dma_start(out=groups[g][tag][:, :, lo:hi], in_=src.rearrange("(p j) w -> p j w", j=4))
 
         def load_group(g):
-            h, c = divmod(g, PASSES)
-            rows = slice(c * 512, (c + 1) * 512)
-            cols = slice(h * HALF, (h + 1) * HALF)
-            tiles = []
-            for tag, src in (("J", J), ("K", mask), ("W", weights)):
-                t = rawp.tile([P, 4, HALF], BF16, tag=tag, name="raw%s%d" % (tag, g))
-                nc.sync.dma_start(out=t[:], in_=src[rows, cols].rearrange("(p j) w -> p j w", j=4))
-                tiles.append(t)
-            return tiles
+            alloc_group(g)
+            for tag in ("J", "K", "W"):
+                load_piece(g, tag, 0, HALF)
 
-        groups = {}
-        groups[0] = load_group(0)
-        groups[1] = load_group(1)
+        st_sb = [const.tile([P, N], BF16, name="st%d" % mt) for mt in range(M_TILES)]
+        noise_sb = [const.tile([P, N], BF16, name="noise%d" % mt) for mt in range(M_TILES)]
 
-        noise_sb = []
+        alloc_group(0)
+        for tag in ("J", "K", "W"):
+            load_piece(0, tag, 0, UNIT)
         for mt in range(M_TILES):
-            t = const.tile([P, N], BF16, name="noise%d" % mt)
-            nc.sync.dma_start(out=t[:], in_=noise_raw[mt * P:(mt + 1) * P, :])
-            noise_sb.append(t)
+            nc.sync.dma_start(out=st_sb[mt][:], in_=state[mt * P:(mt + 1) * P, :])
+        for tag in ("J", "K", "W"):
+            load_piece(0, tag, UNIT, HALF)
+        load_group(1)
+        for mt in range(M_TILES):
+            nc.sync.dma_start(out=noise_sb[mt][:], in_=noise_raw[mt * P:(mt + 1) * P, :])
+        load_group(2)
 
         def small(name, dt=F32):
             return const.tile([P, 16], dt, name=name)
 
         lam32 = const.tile([P, 1], F32, name="lam32")
-        nc.vector.tensor_copy(out=lam32[:], in_=lam_bf[:])
         k_i = small("k_i", I32)
-        nc.vector.tensor_scalar(out=k_i[:], in0=th_bf[:], scalar1=2.0 / math.pi, scalar2=None, op0=ALU.mult)
         k_f = small("k_f")
-        nc.vector.tensor_copy(out=k_f[:], in_=k_i[:])
         x2 = small("x2")
-        nc.vector.tensor_scalar(out=x2[:], in0=th_bf[:], scalar1=2.0, scalar2=None, op0=ALU.mult)
         r1 = small("r1")
-        nc.vector.scalar_tensor_tensor(out=r1[:], in0=k_f[:], scalar=-PI_HI, in1=x2[:], op0=ALU.mult, op1=ALU.add)
         r2 = small("r2")
-        nc.vector.scalar_tensor_tensor(out=r2[:], in0=k_f[:], scalar=-PI_LO, in1=r1[:], op0=ALU.mult, op1=ALU.add)
         a_abs = small("a_abs")
-        nc.vector.scalar_tensor_tensor(out=a_abs[:], in0=r2[:], scalar=-1.0, in1=r2[:], op0=ALU.mult, op1=ALU.max)
         a_ref = small("a_ref")
-        nc.vector.tensor_scalar(out=a_ref[:], in0=a_abs[:], scalar1=-1.0, scalar2=math.pi, op0=ALU.mult, op1=ALU.add)
         a_min = small("a_min")
-        nc.vector.tensor_tensor(out=a_min[:], in0=a_abs[:], in1=a_ref[:], op=ALU.min)
         z = small("z")
-        nc.vector.tensor_tensor(out=z[:], in0=a_min[:], in1=a_min[:], op=ALU.mult)
         a01 = small("a01")
-        nc.vector.tensor_scalar(out=a01[:], in0=a_min[:], scalar1=0.1, scalar2=None, op0=ALU.mult)
-        w = small("w7")
-        nc.vector.tensor_scalar(out=w[:], in0=z[:], scalar1=SIN_COEF[7], scalar2=None, op0=ALU.mult)
-        for k in range(6, 0, -1):
-            w_next = small("w%d" % k)
-            nc.vector.scalar_tensor_tensor(out=w_next[:], in0=w[:], scalar=SIN_COEF[k], in1=z[:], op0=ALU.add, op1=ALU.mult)
-            w = w_next
+        ws = [small("w%d" % k) for k in range(8)]
         tq = small("tq")
-        nc.vector.scalar_tensor_tensor(out=tq[:], in0=w[:], scalar=1.0, in1=a01[:], op0=ALU.add, op1=ALU.mult)
+        V = nc.vector
+        chain = [
+            lambda: V.tensor_copy(out=lam32[:], in_=lam_bf[:]),
+            lambda: V.tensor_scalar(out=k_i[:], in0=th_bf[:], scalar1=2.0 / math.pi, scalar2=None, op0=ALU.mult),
+            lambda: V.tensor_copy(out=k_f[:], in_=k_i[:]),
+            lambda: V.tensor_scalar(out=x2[:], in0=th_bf[:], scalar1=2.0, scalar2=None, op0=ALU.mult),
+            lambda: V.scalar_tensor_tensor(out=r1[:], in0=k_f[:], scalar=-PI_HI, in1=x2[:], op0=ALU.mult, op1=ALU.add),
+            lambda: V.scalar_tensor_tensor(out=r2[:], in0=k_f[:], scalar=-PI_LO, in1=r1[:], op0=ALU.mult, op1=ALU.add),
+            lambda: V.scalar_tensor_tensor(out=a_abs[:], in0=r2[:], scalar=-1.0, in1=r2[:], op0=ALU.mult, op1=ALU.max),
+            lambda: V.tensor_scalar(out=a_ref[:], in0=a_abs[:], scalar1=-1.0, scalar2=math.pi, op0=ALU.mult, op1=ALU.add),
+            lambda: V.tensor_tensor(out=a_min[:], in0=a_abs[:], in1=a_ref[:], op=ALU.min),
+            lambda: V.tensor_tensor(out=z[:], in0=a_min[:], in1=a_min[:], op=ALU.mult),
+            lambda: V.tensor_scalar(out=a01[:], in0=a_min[:], scalar1=0.1, scalar2=None, op0=ALU.mult),
+            lambda: V.tensor_scalar(out=ws[7][:], in0=z[:], scalar1=SIN_COEF[7], scalar2=None, op0=ALU.mult),
+        ]
+
+        def horner(k):
+            return lambda: V.scalar_tensor_tensor(
+                out=ws[k][:], in0=ws[k + 1][:], scalar=SIN_COEF[k], in1=z[:], op0=ALU.add, op1=ALU.mult
+            )
+
+        for k in range(6, 0, -1):
+            chain.append(horner(k))
+        chain.append(
+            lambda: V.scalar_tensor_tensor(out=tq[:], in0=ws[1][:], scalar=1.0, in1=a01[:], op0=ALU.add, op1=ALU.mult)
+        )
+
+        tbs = []
+
+        def spread_t():
+            for b in range(4):
+                tb = psum.tile([P, 512], F32, tag="bank%d" % (4 + b), name="tb%d" % b)
+                for i in range(4):
+                    nc.tensor.matmul(
+                        out=tb[:, i * P:(i + 1) * P],
+                        lhsT=tq[:, 4 * b + i:4 * b + i + 1].to_broadcast([P, P]),
+                        rhs=ident[:],
+                        start=True,
+                        stop=True,
+                    )
+                tbs.append(tb)
+
+        chain_pos = {"n": 0}
+
+        def run_chain(count):
+            for step in range(count):
+                if chain_pos["n"] < len(chain):
+                    chain[chain_pos["n"]]()
+                    chain_pos["n"] += 1
+                    if chain_pos["n"] == len(chain):
+                        spread_t()
 
         s32 = []
         for mt in range(M_TILES):
@@ -130,104 +191,183 @@ def tile_brainquantumlayer_pb_kernel(tc, state, weights, J, theta, lam, mask, no
         s_scales = const.tile([P, PASSES * M_ROWS], U8, name="s_scales", align_bytes=64)
 
         words = [st_sb[mt][:].bitcast(F32).rearrange("m (c v u) -> m c u v", c=PASSES, u=2) for mt in range(M_TILES)]
-        xts = []
+        g_s = []
+        g_st = []
         for c in range(PASSES):
             xt = psum.tile([P, 512], F32, tag="bank%d" % c, name="xt%d" % c)
             xt3 = xt[:].rearrange("p (u m) -> p u m", u=2)
             for mt in range(M_TILES):
                 for u in range(2):
                     nc.tensor.transpose(out=xt3[:, u, mt * P:(mt + 1) * P], in_=words[mt][:, c, u, :], identity=ident[:])
-            xts.append(xt)
-        for c in range(PASSES):
-            xt = xts[c]
-            cs = slice(c * M_ROWS, (c + 1) * M_ROWS)
-            g_s = grpp.tile([P, 1024], BF16, tag="grp", name="g_s%d" % c, align_bytes=64)
+            gs = const.tile([P, 1024], BF16, name="g_s%d" % c, align_bytes=64)
             nc.scalar.activation(
-                out=g_s[:].rearrange("p (m u e) -> p m u e", u=2, e=2),
+                out=gs[:].rearrange("p (m u e) -> p m u e", u=2, e=2),
                 in_=xt[:].bitcast(BF16).rearrange("p (u m e) -> p m u e", u=2, e=2),
                 func=ACT.Tanh,
             )
-            g_st = grpp.tile([P, 1024], BF16, tag="grp", name="g_st%d" % c, align_bytes=64)
-            nc.vector.tensor_copy(
-                out=g_st[:].bitcast(F32).rearrange("p (m u) -> p m u", u=2),
+            gt = const.tile([P, 1024], BF16, name="g_st%d" % c, align_bytes=64)
+            nc.scalar.copy(
+                out=gt[:].bitcast(F32).rearrange("p (m u) -> p m u", u=2),
                 in_=xt[:].rearrange("p (u m) -> p m u", u=2),
             )
-            nc.vector.quantize_mx(out=s_codes[:, cs].bitcast(FP8X4), scales=s_scales[:, cs], in_=g_s[:])
-            nc.vector.quantize_mx(out=st_codes[:, cs].bitcast(FP8X4), scales=st_scales[:, cs], in_=g_st[:])
+            g_s.append(gs)
+            g_st.append(gt)
+
+        done = set()
+
+        def quant_state(c):
+            cs = slice(c * M_ROWS, (c + 1) * M_ROWS)
+            nc.vector.quantize_mx(out=s_codes[:, cs].bitcast(FP8X4), scales=s_scales[:, cs], in_=g_s[c][:])
+            nc.vector.quantize_mx(out=st_codes[:, cs].bitcast(FP8X4), scales=st_scales[:, cs], in_=g_st[c][:])
+            done.add(("a", c))
 
         acc = {}
-        for b in range(4):
-            tb = psum.tile([P, 512], F32, tag="bank%d" % (4 + b), name="tb%d" % b)
-            for i in range(4):
-                nc.tensor.matmul(
-                    out=tb[:, i * P:(i + 1) * P],
-                    lhsT=tq[:, 4 * b + i:4 * b + i + 1].to_broadcast([P, P]),
-                    rhs=ident[:],
-                    start=True,
-                    stop=True,
-                )
+
+        def noise_term(b):
             for mt in range(M_TILES):
                 a = const.tile([P, UNIT], F32, name="acc%d%d" % (mt, b))
                 nc.vector.tensor_tensor(
                     out=a[:].rearrange("q (p i) -> q p i", i=4),
                     in0=noise_sb[mt][:, b * UNIT:(b + 1) * UNIT].rearrange("q (p i) -> q p i", i=4),
-                    in1=tb[:].rearrange("q (i p) -> q p i", i=4),
+                    in1=tbs[b][:].rearrange("q (i p) -> q p i", i=4),
                     op=ALU.mult,
                 )
                 acc[(mt, b)] = a
+            done.add(("pre", b))
 
-        unit_no = 0
+        prods = {}
+        grps = {}
+        codes = {}
         banks = {}
-        for g in range(2 * PASSES):
+
+        def mult(u):
+            g, mat, ntp = units[u]
+            sl = slice(ntp * UNIT, (ntp + 1) * UNIT)
+            raw = groups[g]["W" if mat else "J"]
+            prod = prodp.tile([P, 4, UNIT], BF16, tag="prod", name="prod%d" % u)
+            nc.vector.tensor_tensor(out=prod[:], in0=raw[:, :, sl], in1=groups[g]["K"][:, :, sl], op=ALU.mult)
+            prods[u] = prod
+            run_chain(1)
+            if u % 4 == 3 and g + RAW_BUFS < 2 * PASSES:
+                load_group(g + RAW_BUFS)
+
+        def regroup(u):
+            grp = grpp.tile([P, 4 * UNIT], BF16, tag="grp", name="grp%d" % u, align_bytes=64)
+            dst = grp[:].rearrange("p (c i t) -> p c t i", i=4, t=4)
+            src = prods[u][:].rearrange("p t (c i) -> p c t i", i=4)
+            if u in VECTOR_REGROUPS:
+                nc.vector.tensor_copy(out=dst, in_=src)
+            else:
+                nc.scalar.copy(out=dst, in_=src)
+            grps[u] = grp
+
+        def quant(u):
+            cd = codep.tile([P, UNIT], U32, tag="codes", name="codes%d" % u, align_bytes=64)
+            sc = codep.tile([P, UNIT], U8, tag="scl", name="scl%d" % u, align_bytes=64)
+            nc.vector.quantize_mx(out=cd[:].bitcast(FP8X4), scales=sc[:], in_=grps[u][:])
+            codes[u] = (cd, sc)
+
+        def mx_may_go(u):
+            g, mat, ntp = units[u]
             h, c = divmod(g, PASSES)
-            if g + 2 < 2 * PASSES and g + 2 not in groups:
-                groups[g + 2] = load_group(g + 2)
-            jr, kr, wr = groups[g]
-            for mat, raw in ((0, jr), (1, wr)):
-                a_codes, a_scales = (s_codes, s_scales) if mat == 0 else (st_codes, st_scales)
-                for ntp in range(2):
-                    sl = slice(ntp * UNIT, (ntp + 1) * UNIT)
-                    nt = 2 * h + ntp
-                    prod = prodp.tile([P, 4, UNIT], BF16, tag="prod", name="prod%d" % unit_no)
-                    nc.vector.tensor_tensor(out=prod[:], in0=raw[:, :, sl], in1=kr[:, :, sl], op=ALU.mult)
-                    grp = grpp.tile([P, 4 * UNIT], BF16, tag="grp", name="grp%d" % unit_no, align_bytes=64)
-                    dst = grp[:].rearrange("p (c i t) -> p c t i", i=4, t=4)
-                    src = prod[:].rearrange("p t (c i) -> p c t i", i=4)
-                    if unit_no in VECTOR_REGROUPS:
-                        nc.vector.tensor_copy(out=dst, in_=src)
-                    else:
-                        nc.scalar.copy(out=dst, in_=src)
-                    codes = codep.tile([P, UNIT], U32, tag="codes", name="codes%d" % unit_no, align_bytes=64)
-                    scl = codep.tile([P, UNIT], U8, tag="scl", name="scl%d" % unit_no, align_bytes=64)
-                    nc.vector.quantize_mx(out=codes[:].bitcast(FP8X4), scales=scl[:], in_=grp[:])
-                    for mt in range(M_TILES):
-                        idx = mat * 4 + mt * 2 + ntp
-                        if c == 0:
-                            banks[idx] = psum.tile([P, UNIT], F32, tag="bank%d" % idx, name="acc_ps%d_%d" % (h, idx))
-                        ms = slice(c * M_ROWS + mt * P, c * M_ROWS + (mt + 1) * P)
-                        nc.tensor.matmul_mx(
-                            out=banks[idx][:],
-                            lhsT=a_codes[:, ms].bitcast(FP8X4),
-                            lhsT_scale=a_scales[:, ms],
-                            rhs=codes[:].bitcast(FP8X4),
-                            rhs_scale=scl[:],
-                            start=(c == 0),
-                            stop=(c == PASSES - 1),
-                        )
-                    if c == PASSES - 1:
-                        ns = slice(nt * UNIT, (nt + 1) * UNIT)
-                        for mt in range(M_TILES):
-                            idx = mat * 4 + mt * 2 + ntp
-                            a = acc[(mt, nt)]
-                            if mat == 0:
-                                tmp = tmpp.tile([P, UNIT], F32, tag="tmp", name="tmp%d%d" % (mt, nt))
-                                nc.vector.scalar_tensor_tensor(
-                                    out=tmp[:], in0=banks[idx][:], scalar=lam32[:, 0:1], in1=s32[mt][:, ns],
-                                    op0=ALU.mult, op1=ALU.mult,
-                                )
-                                nc.vector.tensor_tensor(out=a[:], in0=tmp[:], in1=a[:], op=ALU.add)
-                            else:
-                                nc.vector.tensor_tensor(out=a[:], in0=banks[idx][:], in1=a[:], op=ALU.add)
-                                nc.scalar.activation(out=a[:], in_=a[:], func=ACT.Tanh)
-                                nc.sync.dma_start(out=out[mt * P:(mt + 1) * P, ns], in_=a[:])
-                    unit_no += 1
+            if ("a", c) not in done:
+                return False
+            if c == 0 and h == 0 and mat == 1:
+                return all(("pre", b) in done for b in range(4))
+            if c == 0 and h == 1:
+                return ("vec", 0, mat, ntp) in done
+            return True
+
+        def mx(u):
+            g, mat, ntp = units[u]
+            h, c = divmod(g, PASSES)
+            a_codes, a_scales = (st_codes, st_scales) if mat else (s_codes, s_scales)
+            cd, sc = codes[u]
+            for mt in range(M_TILES):
+                idx = mat * 4 + mt * 2 + ntp
+                if c == 0:
+                    banks[idx] = psum.tile([P, UNIT], F32, tag="bank%d" % idx, name="ps%d_%d" % (h, idx))
+                ms = slice(c * M_ROWS + mt * P, c * M_ROWS + (mt + 1) * P)
+                nc.tensor.matmul_mx(
+                    out=banks[idx][:],
+                    lhsT=a_codes[:, ms].bitcast(FP8X4),
+                    lhsT_scale=a_scales[:, ms],
+                    rhs=cd[:].bitcast(FP8X4),
+                    rhs_scale=sc[:],
+                    start=(c == 0),
+                    stop=(c == PASSES - 1),
+                )
+            done.add(("mx", u))
+
+        def vec_epilogue(u):
+            g, mat, ntp = units[u]
+            h = g // PASSES
+            nt = 2 * h + ntp
+            ns = slice(nt * UNIT, (nt + 1) * UNIT)
+            if mat == 0:
+                tmps = []
+                for mt in range(M_TILES):
+                    tmp = tmpp.tile([P, UNIT], F32, tag="tmp", name="tmp%d%d" % (mt, nt))
+                    nc.vector.scalar_tensor_tensor(
+                        out=tmp[:], in0=banks[mt * 2 + ntp][:], scalar=lam32[:, 0:1], in1=s32[mt][:, ns],
+                        op0=ALU.mult, op1=ALU.mult,
+                    )
+                    tmps.append(tmp)
+                for mt in range(M_TILES):
+                    a = acc[(mt, nt)]
+                    nc.vector.tensor_tensor(out=a[:], in0=tmps[mt][:], in1=a[:], op=ALU.add)
+            else:
+                for mt in range(M_TILES):
+                    a = acc[(mt, nt)]
+                    nc.vector.tensor_tensor(out=a[:], in0=banks[4 + mt * 2 + ntp][:], in1=a[:], op=ALU.add)
+            done.add(("vec", h, mat, ntp))
+            done.add(("vecu", u))
+
+        def act_epilogue(u):
+            g, mat, ntp = units[u]
+            nt = 2 * (g // PASSES) + ntp
+            ns = slice(nt * UNIT, (nt + 1) * UNIT)
+            for mt in range(M_TILES):
+                a = acc[(mt, nt)]
+                nc.scalar.activation(out=a[:], in_=a[:], func=ACT.Tanh)
+                nc.sync.dma_start(out=out[mt * P:(mt + 1) * P, ns], in_=a[:])
+            done.add(("actu", u))
+
+        run_chain(CHAIN_FIRST)
+        counters = {"m": 0, "q": 0, "x": 0}
+
+        def mults_to(last):
+            while counters["m"] <= min(last, UNITS - 1):
+                mult(counters["m"])
+                counters["m"] += 1
+
+        def mx_catch_up():
+            while counters["x"] < counters["q"] and mx_may_go(counters["x"]):
+                mx(counters["x"])
+                counters["x"] += 1
+
+        def quants_to(last):
+            while counters["q"] <= min(last, UNITS - 1):
+                quant(counters["q"])
+                counters["q"] += 1
+                mx_catch_up()
+
+        closing = [u for u in range(UNITS) if units[u][0] % PASSES == PASSES - 1]
+        for i in range(UNITS + 12):
+            if i < UNITS:
+                mults_to(i)
+                regroup(i)
+            quants_to(i - 1)
+            mx_catch_up()
+            for u in closing:
+                if u <= i - lag_vec(i) and ("vecu", u) not in done and ("mx", u) in done:
+                    vec_epilogue(u)
+            if 4 <= i < 8:
+                quant_state(i - 4)
+            if 8 <= i < 12:
+                noise_term(i - 8)
+            mults_to(i + lead(i))
+            for u in closing:
+                if units[u][1] == 1 and u <= i - lag_act(i) and ("actu", u) not in done and ("vecu", u) in done:
+                    act_epilogue(u)
+            mx_catch_up()

@@ -18,8 +18,9 @@ M_ROWS = 256
 N = 2048
 M_TILES = 2
 PASSES = 4
-HALF = 1024
 UNIT = 512
+SWEEPS = 4
+UNITS = 32
 
 FLOPS = 2 * 2 * M_ROWS * N * N
 
@@ -27,25 +28,24 @@ PI_HI = 3.140625
 PI_LO = math.pi - PI_HI
 SIN_COEF = (1.0, -1.0 / 6.0, 1.0 / 120.0, -1.0 / 5040.0, 1.0 / 362880.0, -1.0 / 39916800.0, 1.0 / 6227020800.0, -1.0 / 1307674368000.0)
 
-VECTOR_REGROUPS = (0, 1, 2, 3)
+VECTOR_REGROUPS = (2, 8, 9, 17, 25, 29)
+LEAD = 2
+QLAG = 2
+SPLIT = {0: 256, 31: 256}
+NOISE0 = 7
+TANH0 = 8
+STATE_BEHIND = 1
+NOISE_PASS = 2
+ST0 = 2
+NOISE_STEP = 0
+SCALE_STEP = 3
+TANH_STEP = 3
+FIN_LAG = 4
+DLAG = 0
 PROD_BUFS = 6
 GRP_BUFS = 5
-CODE_BUFS = 10
-RAW_BUFS = 3
-UNITS = 32
-CHAIN_FIRST = 12
-
-
-def lead(i):
-    return 1 if i < 3 else (2 if i < 7 else 4)
-
-
-def lag_vec(i):
-    return 5 if i < 28 else 2
-
-
-def lag_act(i):
-    return 8 if i < 28 else 3
+CODE_BUFS = 8
+RAW_BUFS = 6
 
 
 def tile_brainquantumlayer_pb_kernel(tc, state, weights, J, theta, lam, mask, noise_raw, out):
@@ -56,63 +56,92 @@ def tile_brainquantumlayer_pb_kernel(tc, state, weights, J, theta, lam, mask, no
         prodp = ctx.enter_context(tc.tile_pool(name="prod", bufs=PROD_BUFS))
         grpp = ctx.enter_context(tc.tile_pool(name="grp", bufs=GRP_BUFS))
         codep = ctx.enter_context(tc.tile_pool(name="code", bufs=CODE_BUFS))
-        tmpp = ctx.enter_context(tc.tile_pool(name="tmp", bufs=2))
+        sgp = ctx.enter_context(tc.tile_pool(name="sg", bufs=2))
+        ntp_pool = ctx.enter_context(tc.tile_pool(name="ntpool", bufs=2))
+        tmpp = ctx.enter_context(tc.tile_pool(name="tmp", bufs=4))
         psum = ctx.enter_context(tc.psum_pool(name="psum", bufs=1))
         ctx.enter_context(tc.manual_schedule())
 
-        units = []
-        for g in range(2 * PASSES):
-            order = ((0, 0), (1, 0), (0, 1), (1, 1)) if g == 0 else ((0, 0), (0, 1), (1, 0), (1, 1))
-            for mat, ntp in order:
-                units.append((g, mat, ntp))
+        units = [(0, c, mat) for c in range(PASSES) for mat in range(2)]
+        units += [(q, c, mat) for q in range(1, SWEEPS) for mat in range(2) for c in range(PASSES)]
+        index = {(q, mat): max(u for u in range(UNITS) if units[u][0] == q and units[u][2] == mat) for q in range(SWEEPS) for mat in range(2)}
 
+        def unit(u):
+            return units[u]
+
+        theta_rows = const.tile([P, P], BF16, name="theta_rows")
+        nc.gpsimd.memset(theta_rows[:], 0.0)
         ident = const.tile([P, P], F32, name="ident")
         make_identity(nc, ident[:])
-        th_bf = const.tile([P, 16], BF16, name="th_bf")
-        nc.scalar.dma_start(
-            out=th_bf[:].rearrange("p (b i) -> p b i", i=4),
-            in_=theta.rearrange("(b p i) -> p b i", b=4, i=4),
-        )
+        ident_bf = const.tile([P, P], BF16, name="ident_bf")
+        nc.gpsimd.tensor_copy(out=ident_bf[:], in_=ident[:])
+        nc.scalar.dma_start(out=theta_rows[0:16, :], in_=theta.rearrange("(b p) -> b p", b=16))
         lam_bf = const.tile([P, 1], BF16, name="lam_bf")
         nc.scalar.dma_start(out=lam_bf[:], in_=lam.partition_broadcast(P))
 
         sources = {"J": J, "K": mask, "W": weights}
-        groups = {}
+        raws = {}
 
-        def alloc_group(g):
-            groups[g] = {}
-            for tag in ("J", "K", "W"):
-                groups[g][tag] = rawp.tile([P, 4, HALF], BF16, tag=tag, name="raw%s%d" % (tag, g))
-
-        def load_piece(g, tag, lo, hi):
-            h, c = divmod(g, PASSES)
-            src = sources[tag][c * 512:(c + 1) * 512, h * HALF + lo:h * HALF + hi]
-            nc.sync.dma_start(out=groups[g][tag][:, :, lo:hi], in_=src.rearrange("(p j) w -> p j w", j=4))
-
-        def load_group(g):
-            alloc_group(g)
-            for tag in ("J", "K", "W"):
-                load_piece(g, tag, 0, HALF)
+        def load_raw(q, c, tag, lo=0, hi=UNIT):
+            if (q, c, tag) not in raws:
+                raws[(q, c, tag)] = rawp.tile([P, 4, UNIT], BF16, tag=tag, name="raw%s%d%d" % (tag, q, c))
+            src = sources[tag][c * 512:(c + 1) * 512, q * UNIT + lo:q * UNIT + hi]
+            nc.sync.dma_start(out=raws[(q, c, tag)][:, :, lo:hi], in_=src.rearrange("(p j) w -> p j w", j=4))
 
         st_sb = [const.tile([P, N], BF16, name="st%d" % mt) for mt in range(M_TILES)]
         noise_sb = [const.tile([P, N], BF16, name="noise%d" % mt) for mt in range(M_TILES)]
 
-        alloc_group(0)
-        for tag in ("J", "K", "W"):
-            load_piece(0, tag, 0, UNIT)
-        for mt in range(M_TILES):
-            nc.sync.dma_start(out=st_sb[mt][:], in_=state[mt * P:(mt + 1) * P, :])
-        for tag in ("J", "K", "W"):
-            load_piece(0, tag, UNIT, HALF)
-        load_group(1)
-        for mt in range(M_TILES):
-            nc.sync.dma_start(out=noise_sb[mt][:], in_=noise_raw[mt * P:(mt + 1) * P, :])
-        load_group(2)
+        def load_state(c):
+            for mt in range(M_TILES):
+                nc.sync.dma_start(out=st_sb[mt][:, c * UNIT:(c + 1) * UNIT], in_=state[mt * P:(mt + 1) * P, c * UNIT:(c + 1) * UNIT])
+
+        def load_noise(q):
+            for mt in range(M_TILES):
+                nc.sync.dma_start(out=noise_sb[mt][:, q * UNIT:(q + 1) * UNIT], in_=noise_raw[mt * P:(mt + 1) * P, q * UNIT:(q + 1) * UNIT])
+
+        loads = []
+        for c in range(PASSES):
+            loads += [("J", 0, c), ("K", 0, c), ("W", 0, c)]
+            if c >= STATE_BEHIND:
+                loads.append(("state", 0, c - STATE_BEHIND))
+            if c == NOISE_PASS:
+                loads.append(("noise", 0, 0))
+        for q in range(1, SWEEPS):
+            for c in range(PASSES):
+                loads += [("J", q, c), ("K", q, c)]
+                if q == 1 and c < STATE_BEHIND:
+                    loads.append(("state", 0, PASSES - STATE_BEHIND + c))
+            loads.append(("noise", q, 0))
+            loads += [("W", q, c) for c in range(PASSES)]
+        used = {"J": 0, "K": 0, "W": 0}
+        issued = {"J": 0, "K": 0, "W": 0}
+
+        def load_on():
+            while loads:
+                tag, q, c = loads[0]
+                if tag == "state":
+                    load_state(c)
+                elif tag == "noise":
+                    load_noise(q)
+                else:
+                    if issued[tag] - used[tag] >= RAW_BUFS:
+                        return
+                    issued[tag] += 1
+                    if (q, c) == (0, 0) and tag == "J":
+                        for lo in (0, 256):
+                            load_raw(q, c, "J", lo, lo + 256)
+                            load_raw(q, c, "K", lo, lo + 256)
+                    elif (q, c) != (0, 0) or tag != "K":
+                        load_raw(q, c, tag)
+                loads.remove(loads[0])
+
+        load_on()
 
         def small(name, dt=F32):
             return const.tile([P, 16], dt, name=name)
 
         lam32 = const.tile([P, 1], F32, name="lam32")
+        th = small("th")
         k_i = small("k_i", I32)
         k_f = small("k_f")
         x2 = small("x2")
@@ -123,14 +152,17 @@ def tile_brainquantumlayer_pb_kernel(tc, state, weights, J, theta, lam, mask, no
         a_min = small("a_min")
         z = small("z")
         a01 = small("a01")
-        ws = [small("w%d" % k) for k in range(8)]
+        ws = {k: small("w%d" % k) for k in range(1, 8)}
         tq = small("tq")
         V = nc.vector
+        th_ps = psum.tile([P, P], BF16, tag="bank7", name="th_ps")
+        nc.tensor.transpose(out=th_ps[:], in_=theta_rows[:], identity=ident_bf[:])
         chain = [
             lambda: V.tensor_copy(out=lam32[:], in_=lam_bf[:]),
-            lambda: V.tensor_scalar(out=k_i[:], in0=th_bf[:], scalar1=2.0 / math.pi, scalar2=None, op0=ALU.mult),
+            lambda: V.tensor_copy(out=th[:], in_=th_ps[:, 0:16]),
+            lambda: V.tensor_scalar(out=k_i[:], in0=th[:], scalar1=2.0 / math.pi, scalar2=None, op0=ALU.mult),
             lambda: V.tensor_copy(out=k_f[:], in_=k_i[:]),
-            lambda: V.tensor_scalar(out=x2[:], in0=th_bf[:], scalar1=2.0, scalar2=None, op0=ALU.mult),
+            lambda: V.tensor_scalar(out=x2[:], in0=th[:], scalar1=2.0, scalar2=None, op0=ALU.mult),
             lambda: V.scalar_tensor_tensor(out=r1[:], in0=k_f[:], scalar=-PI_HI, in1=x2[:], op0=ALU.mult, op1=ALU.add),
             lambda: V.scalar_tensor_tensor(out=r2[:], in0=k_f[:], scalar=-PI_LO, in1=r1[:], op0=ALU.mult, op1=ALU.add),
             lambda: V.scalar_tensor_tensor(out=a_abs[:], in0=r2[:], scalar=-1.0, in1=r2[:], op0=ALU.mult, op1=ALU.max),
@@ -151,22 +183,6 @@ def tile_brainquantumlayer_pb_kernel(tc, state, weights, J, theta, lam, mask, no
         chain.append(
             lambda: V.scalar_tensor_tensor(out=tq[:], in0=ws[1][:], scalar=1.0, in1=a01[:], op0=ALU.add, op1=ALU.mult)
         )
-
-        tbs = []
-
-        def spread_t():
-            for b in range(4):
-                tb = psum.tile([P, 512], F32, tag="bank%d" % (4 + b), name="tb%d" % b)
-                for i in range(4):
-                    nc.tensor.matmul(
-                        out=tb[:, i * P:(i + 1) * P],
-                        lhsT=tq[:, 4 * b + i:4 * b + i + 1].to_broadcast([P, P]),
-                        rhs=ident[:],
-                        start=True,
-                        stop=True,
-                    )
-                tbs.append(tb)
-
         chain_pos = {"n": 0}
 
         def run_chain(count):
@@ -174,66 +190,66 @@ def tile_brainquantumlayer_pb_kernel(tc, state, weights, J, theta, lam, mask, no
                 if chain_pos["n"] < len(chain):
                     chain[chain_pos["n"]]()
                     chain_pos["n"] += 1
-                    if chain_pos["n"] == len(chain):
-                        spread_t()
 
-        s32 = []
-        for mt in range(M_TILES):
-            t = const.tile([P, N], F32, name="s32_%d" % mt)
-            for q in range(2):
-                sl = slice(q * HALF, (q + 1) * HALF)
-                nc.scalar.activation(out=t[:, sl], in_=st_sb[mt][:, sl], func=ACT.Tanh)
-            s32.append(t)
-
-        st_codes = const.tile([P, PASSES * M_ROWS], U32, name="st_codes", align_bytes=64)
-        st_scales = const.tile([P, PASSES * M_ROWS], U8, name="st_scales", align_bytes=64)
-        s_codes = const.tile([P, PASSES * M_ROWS], U32, name="s_codes", align_bytes=64)
-        s_scales = const.tile([P, PASSES * M_ROWS], U8, name="s_scales", align_bytes=64)
-
-        words = [st_sb[mt][:].bitcast(F32).rearrange("m (c v u) -> m c u v", c=PASSES, u=2) for mt in range(M_TILES)]
-        g_s = []
-        g_st = []
-        for c in range(PASSES):
-            xt = psum.tile([P, 512], F32, tag="bank%d" % c, name="xt%d" % c)
-            xt3 = xt[:].rearrange("p (u m) -> p u m", u=2)
-            for mt in range(M_TILES):
-                for u in range(2):
-                    nc.tensor.transpose(out=xt3[:, u, mt * P:(mt + 1) * P], in_=words[mt][:, c, u, :], identity=ident[:])
-            gs = const.tile([P, 1024], BF16, name="g_s%d" % c, align_bytes=64)
-            nc.scalar.activation(
-                out=gs[:].rearrange("p (m u e) -> p m u e", u=2, e=2),
-                in_=xt[:].bitcast(BF16).rearrange("p (u m e) -> p m u e", u=2, e=2),
-                func=ACT.Tanh,
-            )
-            gt = const.tile([P, 1024], BF16, name="g_st%d" % c, align_bytes=64)
-            nc.scalar.copy(
-                out=gt[:].bitcast(F32).rearrange("p (m u) -> p m u", u=2),
-                in_=xt[:].rearrange("p (u m) -> p m u", u=2),
-            )
-            g_s.append(gs)
-            g_st.append(gt)
-
+        s32 = [const.tile([P, N], F32, name="s32_%d" % mt) for mt in range(M_TILES)]
+        a_codes = const.tile([P, PASSES * 2 * M_ROWS], U32, name="a_codes", align_bytes=64)
+        a_scales = const.tile([P, PASSES * 2 * M_ROWS], U8, name="a_scales", align_bytes=64)
+        g_a = {}
         done = set()
 
+        def turn_state(c):
+            xt = psum.tile([P, 512], F32, tag="bank%d" % (4 + c % 2), name="xt%d" % c)
+            xt3 = xt[:].rearrange("p (u m) -> p u m", u=2)
+            for mt in range(M_TILES):
+                words = st_sb[mt][:, c * UNIT:(c + 1) * UNIT].bitcast(F32).rearrange("m (v u) -> m u v", u=2)
+                for u in range(2):
+                    nc.tensor.transpose(out=xt3[:, u, mt * P:(mt + 1) * P], in_=words[:, u, :], identity=ident[:])
+            return xt
+
+        turned = {}
+
+        def spread_state(c, which):
+            xt = turned[c]
+            if which == 0:
+                g_a[c] = sgp.tile([P, 2048], BF16, tag="g_a", name="g_a%d" % c, align_bytes=64)
+                nc.scalar.activation(
+                    out=g_a[c][:, 0:1024].rearrange("p (m u e) -> p m u e", u=2, e=2),
+                    in_=xt[:].bitcast(BF16).rearrange("p (u m e) -> p m u e", u=2, e=2),
+                    func=ACT.Tanh,
+                )
+            else:
+                nc.scalar.copy(
+                    out=g_a[c][:, 1024:2048].bitcast(F32).rearrange("p (m u) -> p m u", u=2),
+                    in_=xt[:].rearrange("p (u m) -> p m u", u=2),
+                )
+
         def quant_state(c):
-            cs = slice(c * M_ROWS, (c + 1) * M_ROWS)
-            nc.vector.quantize_mx(out=s_codes[:, cs].bitcast(FP8X4), scales=s_scales[:, cs], in_=g_s[c][:])
-            nc.vector.quantize_mx(out=st_codes[:, cs].bitcast(FP8X4), scales=st_scales[:, cs], in_=g_st[c][:])
+            cs = slice(c * 2 * M_ROWS, (c + 1) * 2 * M_ROWS)
+            nc.vector.quantize_mx(out=a_codes[:, cs].bitcast(FP8X4), scales=a_scales[:, cs], in_=g_a[c][:])
             done.add(("a", c))
 
-        acc = {}
-
-        def noise_term(b):
+        def tanh_rows(q):
             for mt in range(M_TILES):
-                a = const.tile([P, UNIT], F32, name="acc%d%d" % (mt, b))
-                nc.vector.tensor_tensor(
-                    out=a[:].rearrange("q (p i) -> q p i", i=4),
-                    in0=noise_sb[mt][:, b * UNIT:(b + 1) * UNIT].rearrange("q (p i) -> q p i", i=4),
-                    in1=tbs[b][:].rearrange("q (i p) -> q p i", i=4),
-                    op=ALU.mult,
-                )
-                acc[(mt, b)] = a
-            done.add(("pre", b))
+                sl = slice(q * UNIT, (q + 1) * UNIT)
+                nc.scalar.activation(out=s32[mt][:, sl], in_=st_sb[mt][:, sl], func=ACT.Tanh)
+
+        nT = {}
+        nps = {}
+
+        def turn_noise(q):
+            nps[q] = psum.tile([P, 4, M_ROWS], BF16, tag="bank6", name="nps%d" % q)
+            for j in range(4):
+                for mt in range(M_TILES):
+                    nc.tensor.transpose(
+                        out=nps[q][:, j, mt * P:(mt + 1) * P],
+                        in_=noise_sb[mt][:, q * UNIT + j * P:q * UNIT + (j + 1) * P],
+                        identity=ident_bf[:],
+                    )
+
+        def scale_noise(q):
+            nT[q] = ntp_pool.tile([P, 4, M_ROWS], F32, tag="nT", name="nT%d" % q)
+            for j in range(4):
+                nc.scalar.activation(out=nT[q][:, j, :], in_=nps[q][:, j, :], func=ACT.Copy, scale=tq[:, 4 * q + j:4 * q + j + 1])
 
         prods = {}
         grps = {}
@@ -241,53 +257,59 @@ def tile_brainquantumlayer_pb_kernel(tc, state, weights, J, theta, lam, mask, no
         banks = {}
 
         def mult(u):
-            g, mat, ntp = units[u]
-            sl = slice(ntp * UNIT, (ntp + 1) * UNIT)
-            raw = groups[g]["W" if mat else "J"]
+            q, c, mat = unit(u)
+            raw = raws[(q, c, "W" if mat else "J")]
             prod = prodp.tile([P, 4, UNIT], BF16, tag="prod", name="prod%d" % u)
-            nc.vector.tensor_tensor(out=prod[:], in0=raw[:, :, sl], in1=groups[g]["K"][:, :, sl], op=ALU.mult)
+            msk = raws[(q, c, "K")]
+            parts = ((0, 256), (256, 512)) if u == 0 else ((0, 512),)
+            for lo, hi in parts:
+                nc.vector.tensor_tensor(out=prod[:, :, lo:hi], in0=raw[:, :, lo:hi], in1=msk[:, :, lo:hi], op=ALU.mult)
             prods[u] = prod
             run_chain(1)
-            if u % 4 == 3 and g + RAW_BUFS < 2 * PASSES:
-                load_group(g + RAW_BUFS)
+            used["W" if mat else "J"] += 1
+            used["K"] += mat
+            load_on()
 
-        def regroup(u):
-            grp = grpp.tile([P, 4 * UNIT], BF16, tag="grp", name="grp%d" % u, align_bytes=64)
-            dst = grp[:].rearrange("p (c i t) -> p c t i", i=4, t=4)
-            src = prods[u][:].rearrange("p t (c i) -> p c t i", i=4)
-            if u in VECTOR_REGROUPS:
+        def regroup_part(u, vector, lo, hi):
+            dst = grps[u][:, 4 * lo:4 * hi].rearrange("p (c i t) -> p c t i", i=4, t=4)
+            src = prods[u][:, :, lo:hi].rearrange("p t (c i) -> p c t i", i=4)
+            if vector:
                 nc.vector.tensor_copy(out=dst, in_=src)
             else:
                 nc.scalar.copy(out=dst, in_=src)
-            grps[u] = grp
+
+        def regroup(u):
+            grps[u] = grpp.tile([P, 4 * UNIT], BF16, tag="grp", name="grp%d" % u, align_bytes=64)
+            if u in SPLIT:
+                regroup_part(u, False, 0, SPLIT[u])
+                regroup_part(u, u > 0, SPLIT[u], UNIT)
+            else:
+                regroup_part(u, u in VECTOR_REGROUPS, 0, UNIT)
 
         def quant(u):
             cd = codep.tile([P, UNIT], U32, tag="codes", name="codes%d" % u, align_bytes=64)
             sc = codep.tile([P, UNIT], U8, tag="scl", name="scl%d" % u, align_bytes=64)
             nc.vector.quantize_mx(out=cd[:].bitcast(FP8X4), scales=sc[:], in_=grps[u][:])
             codes[u] = (cd, sc)
+            run_chain(1)
 
         def mx_may_go(u):
-            g, mat, ntp = units[u]
-            h, c = divmod(g, PASSES)
+            q, c, mat = unit(u)
             if ("a", c) not in done:
                 return False
-            if c == 0 and h == 0 and mat == 1:
-                return all(("pre", b) in done for b in range(4))
-            if c == 0 and h == 1:
-                return ("vec", 0, mat, ntp) in done
+            if c == 0 and q > 0:
+                return ("vec", q - 1, mat) in done
             return True
 
         def mx(u):
-            g, mat, ntp = units[u]
-            h, c = divmod(g, PASSES)
-            a_codes, a_scales = (st_codes, st_scales) if mat else (s_codes, s_scales)
+            q, c, mat = unit(u)
             cd, sc = codes[u]
             for mt in range(M_TILES):
-                idx = mat * 4 + mt * 2 + ntp
+                idx = mat * 2 + mt
                 if c == 0:
-                    banks[idx] = psum.tile([P, UNIT], F32, tag="bank%d" % idx, name="ps%d_%d" % (h, idx))
-                ms = slice(c * M_ROWS + mt * P, c * M_ROWS + (mt + 1) * P)
+                    banks[idx] = psum.tile([P, UNIT], F32, tag="bank%d" % idx, name="ps%d_%d" % (q, idx))
+                lo = (2 * c + mat) * M_ROWS + mt * P
+                ms = slice(lo, lo + P)
                 nc.tensor.matmul_mx(
                     out=banks[idx][:],
                     lhsT=a_codes[:, ms].bitcast(FP8X4),
@@ -299,41 +321,46 @@ def tile_brainquantumlayer_pb_kernel(tc, state, weights, J, theta, lam, mask, no
                 )
             done.add(("mx", u))
 
-        def vec_epilogue(u):
-            g, mat, ntp = units[u]
-            h = g // PASSES
-            nt = 2 * h + ntp
-            ns = slice(nt * UNIT, (nt + 1) * UNIT)
-            if mat == 0:
-                tmps = []
-                for mt in range(M_TILES):
-                    tmp = tmpp.tile([P, UNIT], F32, tag="tmp", name="tmp%d%d" % (mt, nt))
-                    nc.vector.scalar_tensor_tensor(
-                        out=tmp[:], in0=banks[mt * 2 + ntp][:], scalar=lam32[:, 0:1], in1=s32[mt][:, ns],
-                        op0=ALU.mult, op1=ALU.mult,
-                    )
-                    tmps.append(tmp)
-                for mt in range(M_TILES):
-                    a = acc[(mt, nt)]
-                    nc.vector.tensor_tensor(out=a[:], in0=tmps[mt][:], in1=a[:], op=ALU.add)
-            else:
-                for mt in range(M_TILES):
-                    a = acc[(mt, nt)]
-                    nc.vector.tensor_tensor(out=a[:], in0=banks[4 + mt * 2 + ntp][:], in1=a[:], op=ALU.add)
-            done.add(("vec", h, mat, ntp))
-            done.add(("vecu", u))
+        tmps = {}
+        xb = {}
 
-        def act_epilogue(u):
-            g, mat, ntp = units[u]
-            nt = 2 * (g // PASSES) + ntp
-            ns = slice(nt * UNIT, (nt + 1) * UNIT)
+        def gain_delta(q):
             for mt in range(M_TILES):
-                a = acc[(mt, nt)]
-                nc.scalar.activation(out=a[:], in_=a[:], func=ACT.Tanh)
-                nc.sync.dma_start(out=out[mt * P:(mt + 1) * P, ns], in_=a[:])
-            done.add(("actu", u))
+                t = tmpp.tile([P, UNIT], F32, tag="t", name="t%d%d" % (mt, q))
+                nc.vector.scalar_tensor_tensor(
+                    out=t[:], in0=banks[mt][:], scalar=lam32[:, 0:1], in1=s32[mt][:, q * UNIT:(q + 1) * UNIT],
+                    op0=ALU.mult, op1=ALU.mult,
+                )
+                tmps[(mt, q)] = t
+            done.add(("vec", q, 0))
 
-        run_chain(CHAIN_FIRST)
+        def add_noise(q):
+            for mt in range(M_TILES):
+                t = tmps[(mt, q)]
+                nc.vector.tensor_tensor(out=t[:], in0=xb[(mt, q)][:], in1=t[:], op=ALU.add)
+
+        def add_signal(q):
+            for mt in range(M_TILES):
+                t = tmps[(mt, q)]
+                nc.vector.tensor_tensor(out=t[:], in0=banks[2 + mt][:], in1=t[:], op=ALU.add)
+            done.add(("vec", q, 1))
+
+        def join(q, with_t):
+            for mt in range(M_TILES):
+                x = psum.tile([P, UNIT], F32, tag="bank%d" % (7 - mt if q == SWEEPS - 1 else 4 + mt), name="x%d%d" % (mt, q))
+                for j in range(4):
+                    nc.tensor.matmul(out=x[:, j * P:(j + 1) * P], lhsT=nT[q][:, j, mt * P:(mt + 1) * P], rhs=ident[:], start=True, stop=not with_t)
+                    if with_t:
+                        nc.tensor.matmul(out=x[:, j * P:(j + 1) * P], lhsT=ident[:], rhs=tmps[(mt, q)][:, j * P:(j + 1) * P], start=False, stop=True)
+                xb[(mt, q)] = x
+
+        def finish(q):
+            for mt in range(M_TILES):
+                t = tmps[(mt, q)]
+                src = xb[(mt, q)] if q < SWEEPS - 1 else t
+                nc.scalar.activation(out=t[:], in_=src[:], func=ACT.Tanh)
+                nc.sync.dma_start(out=out[mt * P:(mt + 1) * P, q * UNIT:(q + 1) * UNIT], in_=t[:])
+
         counters = {"m": 0, "q": 0, "x": 0}
 
         def mults_to(last):
@@ -352,22 +379,49 @@ def tile_brainquantumlayer_pb_kernel(tc, state, weights, J, theta, lam, mask, no
                 counters["q"] += 1
                 mx_catch_up()
 
-        closing = [u for u in range(UNITS) if units[u][0] % PASSES == PASSES - 1]
-        for i in range(UNITS + 12):
+        stage = [(0, 0) for w in range(SWEEPS)]
+        for i in range(UNITS + 6):
+            q, r = divmod(i, 8)
             if i < UNITS:
                 mults_to(i)
                 regroup(i)
-            quants_to(i - 1)
+            if i < 10:
+                run_chain(1)
+            quants_to(i - QLAG)
             mx_catch_up()
-            for u in closing:
-                if u <= i - lag_vec(i) and ("vecu", u) not in done and ("mx", u) in done:
-                    vec_epilogue(u)
-            if 4 <= i < 8:
-                quant_state(i - 4)
-            if 8 <= i < 12:
-                noise_term(i - 8)
-            mults_to(i + lead(i))
-            for u in closing:
-                if units[u][1] == 1 and u <= i - lag_act(i) and ("actu", u) not in done and ("vecu", u) in done:
-                    act_epilogue(u)
+            e = i - ST0
+            if 0 <= e < 8 and e % 2 == 0:
+                turned[e // 2] = turn_state(e // 2)
+            if 1 <= e < 9:
+                spread_state((e - 1) // 2, (e - 1) % 2)
+            if 2 <= e < 10 and e % 2 == 1:
+                quant_state((e - 3) // 2)
+                mx_catch_up()
+            mults_to(i + LEAD)
+            for w in range(SWEEPS):
+                if i == (8 * w + NOISE_STEP if w else NOISE0):
+                    turn_noise(w)
+                if i == (8 * w + SCALE_STEP if w else NOISE0 + 2):
+                    scale_noise(w)
+                if i == (8 * w + TANH_STEP if w else TANH0):
+                    tanh_rows(w)
+            for w in range(SWEEPS):
+                last = w == SWEEPS - 1
+                if stage[w][0] == 0 and i >= index[(w, 0)] + 2 + DLAG and ("mx", index[(w, 0)]) in done:
+                    gain_delta(w)
+                    if last:
+                        join(w, False)
+                        add_noise(w)
+                    stage[w] = (1, i)
+                elif stage[w][0] == 1 and i > stage[w][1] and ("mx", index[(w, 1)]) in done:
+                    add_signal(w)
+                    stage[w] = (2, i)
+                    if last:
+                        finish(w)
+                elif stage[w][0] == 2 and i > stage[w][1] and not last:
+                    join(w, True)
+                    stage[w] = (3, i)
+                elif stage[w][0] == 3 and i >= stage[w][1] + FIN_LAG:
+                    finish(w)
+                    stage[w] = (4, i)
             mx_catch_up()

@@ -18,8 +18,8 @@ M_ROWS = 256
 N = 2048
 M_TILES = 2
 PASSES = 4
+HALF = 1024
 UNIT = 512
-SWEEPS = 4
 UNITS = 32
 
 FLOPS = 2 * 2 * M_ROWS * N * N
@@ -28,24 +28,34 @@ PI_HI = 3.140625
 PI_LO = math.pi - PI_HI
 SIN_COEF = (1.0, -1.0 / 6.0, 1.0 / 120.0, -1.0 / 5040.0, 1.0 / 362880.0, -1.0 / 39916800.0, 1.0 / 6227020800.0, -1.0 / 1307674368000.0)
 
-VECTOR_REGROUPS = (2, 8, 9, 17, 25, 29)
-LEAD = 2
+VECTOR_REGROUPS = (0, 2, 6, 30)
+TENSOR_REGROUPS = (9, 13, 17, 21, 25)
+J_FIRST = (1, 2, 3)
+STATE_BEHIND = 5
+NOISE_BEHIND = 20
+SPLIT_FIRST = 0
+LEADS = (1, 3, 2, 40, 2)
 QLAG = 2
-SPLIT = {0: 256, 31: 256}
-NOISE0 = 7
-TANH0 = 8
-STATE_BEHIND = 1
-NOISE_PASS = 2
-ST0 = 2
-NOISE_STEP = 0
-SCALE_STEP = 3
-TANH_STEP = 3
-FIN_LAG = 4
-DLAG = 0
-PROD_BUFS = 6
+ST0 = 1
+STD = 2
+STQ = 2
+S_BEFORE = 2
+B_LAG = 3
+A_LAG = 2
+D_LAG = 1
+O_LAG = 1
+F_LAG = 1
+PROD_BUFS = 7
 GRP_BUFS = 5
 CODE_BUFS = 8
 RAW_BUFS = 6
+GA_BUFS = 2
+OUT_BUFS = 2
+CHAIN_FIRST = 0
+
+
+def lead(i):
+    return LEADS[0] if i < LEADS[1] else (LEADS[2] if i < LEADS[3] else LEADS[4])
 
 
 def tile_brainquantumlayer_pb_kernel(tc, state, weights, J, theta, lam, mask, noise_raw, out):
@@ -56,18 +66,19 @@ def tile_brainquantumlayer_pb_kernel(tc, state, weights, J, theta, lam, mask, no
         prodp = ctx.enter_context(tc.tile_pool(name="prod", bufs=PROD_BUFS))
         grpp = ctx.enter_context(tc.tile_pool(name="grp", bufs=GRP_BUFS))
         codep = ctx.enter_context(tc.tile_pool(name="code", bufs=CODE_BUFS))
-        sgp = ctx.enter_context(tc.tile_pool(name="sg", bufs=2))
-        ntp_pool = ctx.enter_context(tc.tile_pool(name="ntpool", bufs=2))
-        tmpp = ctx.enter_context(tc.tile_pool(name="tmp", bufs=4))
+        twop = ctx.enter_context(tc.tile_pool(name="two", bufs=2))
+        onep = ctx.enter_context(tc.tile_pool(name="one", bufs=GA_BUFS))
+        outp = ctx.enter_context(tc.tile_pool(name="outp", bufs=OUT_BUFS))
         psum = ctx.enter_context(tc.psum_pool(name="psum", bufs=1))
         ctx.enter_context(tc.manual_schedule())
 
-        units = [(0, c, mat) for c in range(PASSES) for mat in range(2)]
-        units += [(q, c, mat) for q in range(1, SWEEPS) for mat in range(2) for c in range(PASSES)]
-        index = {(q, mat): max(u for u in range(UNITS) if units[u][0] == q and units[u][2] == mat) for q in range(SWEEPS) for mat in range(2)}
-
-        def unit(u):
-            return units[u]
+        units = []
+        for nt in range(4):
+            if nt in J_FIRST:
+                units += [(nt, c, mat) for mat in range(2) for c in range(PASSES)]
+            else:
+                units += [(nt, c, mat) for c in range(PASSES) for mat in range(2)]
+        last = {(nt, mat): max(u for u in range(UNITS) if units[u][0] == nt and units[u][2] == mat) for nt in range(4) for mat in range(2)}
 
         theta_rows = const.tile([P, P], BF16, name="theta_rows")
         nc.gpsimd.memset(theta_rows[:], 0.0)
@@ -80,59 +91,47 @@ def tile_brainquantumlayer_pb_kernel(tc, state, weights, J, theta, lam, mask, no
         nc.scalar.dma_start(out=lam_bf[:], in_=lam.partition_broadcast(P))
 
         sources = {"J": J, "K": mask, "W": weights}
-        raws = {}
-
-        def load_raw(q, c, tag, lo=0, hi=UNIT):
-            if (q, c, tag) not in raws:
-                raws[(q, c, tag)] = rawp.tile([P, 4, UNIT], BF16, tag=tag, name="raw%s%d%d" % (tag, q, c))
-            src = sources[tag][c * 512:(c + 1) * 512, q * UNIT + lo:q * UNIT + hi]
-            nc.sync.dma_start(out=raws[(q, c, tag)][:, :, lo:hi], in_=src.rearrange("(p j) w -> p j w", j=4))
-
+        groups = {}
         st_sb = [const.tile([P, N], BF16, name="st%d" % mt) for mt in range(M_TILES)]
         noise_sb = [const.tile([P, N], BF16, name="noise%d" % mt) for mt in range(M_TILES)]
 
-        def load_state(c):
+        def load_rows(tiles, source):
             for mt in range(M_TILES):
-                nc.sync.dma_start(out=st_sb[mt][:, c * UNIT:(c + 1) * UNIT], in_=state[mt * P:(mt + 1) * P, c * UNIT:(c + 1) * UNIT])
-
-        def load_noise(q):
-            for mt in range(M_TILES):
-                nc.sync.dma_start(out=noise_sb[mt][:, q * UNIT:(q + 1) * UNIT], in_=noise_raw[mt * P:(mt + 1) * P, q * UNIT:(q + 1) * UNIT])
+                nc.sync.dma_start(out=tiles[mt][:], in_=source[mt * P:(mt + 1) * P, :])
 
         loads = []
-        for c in range(PASSES):
-            loads += [("J", 0, c), ("K", 0, c), ("W", 0, c)]
-            if c >= STATE_BEHIND:
-                loads.append(("state", 0, c - STATE_BEHIND))
-            if c == NOISE_PASS:
-                loads.append(("noise", 0, 0))
-        for q in range(1, SWEEPS):
-            for c in range(PASSES):
-                loads += [("J", q, c), ("K", q, c)]
-                if q == 1 and c < STATE_BEHIND:
-                    loads.append(("state", 0, PASSES - STATE_BEHIND + c))
-            loads.append(("noise", q, 0))
-            loads += [("W", q, c) for c in range(PASSES)]
-        used = {"J": 0, "K": 0, "W": 0}
-        issued = {"J": 0, "K": 0, "W": 0}
+        for nt in range(4):
+            if nt in J_FIRST:
+                part = [(tag, nt, c) for c in range(PASSES) for tag in ("J", "K")] + [("W", nt, c) for c in range(PASSES)]
+            else:
+                part = [(tag, nt, c) for c in range(PASSES) for tag in ("J", "K", "W")]
+            for item in part:
+                loads.append(item)
+                if len(loads) == STATE_BEHIND:
+                    loads.append(("S", 0, 0))
+                if len(loads) == NOISE_BEHIND:
+                    loads.append(("N", 0, 0))
+        free_bufs = {"J": RAW_BUFS, "K": RAW_BUFS, "W": RAW_BUFS}
+        reads_left = {}
 
         def load_on():
             while loads:
-                tag, q, c = loads[0]
-                if tag == "state":
-                    load_state(c)
-                elif tag == "noise":
-                    load_noise(q)
+                tag, nt, c = loads[0]
+                if tag == "S":
+                    load_rows(st_sb, state)
+                elif tag == "N":
+                    load_rows(noise_sb, noise_raw)
                 else:
-                    if issued[tag] - used[tag] >= RAW_BUFS:
+                    if free_bufs[tag] == 0:
                         return
-                    issued[tag] += 1
-                    if (q, c) == (0, 0) and tag == "J":
-                        for lo in (0, 256):
-                            load_raw(q, c, "J", lo, lo + 256)
-                            load_raw(q, c, "K", lo, lo + 256)
-                    elif (q, c) != (0, 0) or tag != "K":
-                        load_raw(q, c, tag)
+                    free_bufs[tag] -= 1
+                    reads_left[(tag, nt, c)] = 2 if tag == "K" else 1
+                    raw = rawp.tile([P, 4, UNIT], BF16, tag=tag, name="raw%s%d%d" % (tag, nt, c))
+                    groups[(tag, nt, c)] = raw
+                    src = sources[tag][c * UNIT:(c + 1) * UNIT, nt * UNIT:(nt + 1) * UNIT]
+                    cuts = (0, 256, 512) if SPLIT_FIRST and (nt, c) == (0, 0) and tag != "W" else (0, 512)
+                    for lo, hi in zip(cuts, cuts[1:]):
+                        nc.sync.dma_start(out=raw[:, :, lo:hi], in_=src.rearrange("(p j) w -> p j w", j=4)[:, :, lo:hi])
                 loads.remove(loads[0])
 
         load_on()
@@ -191,237 +190,238 @@ def tile_brainquantumlayer_pb_kernel(tc, state, weights, J, theta, lam, mask, no
                     chain[chain_pos["n"]]()
                     chain_pos["n"] += 1
 
-        s32 = [const.tile([P, N], F32, name="s32_%d" % mt) for mt in range(M_TILES)]
         a_codes = const.tile([P, PASSES * 2 * M_ROWS], U32, name="a_codes", align_bytes=64)
         a_scales = const.tile([P, PASSES * 2 * M_ROWS], U8, name="a_scales", align_bytes=64)
         g_a = {}
         done = set()
 
-        def turn_state(c):
-            xt = psum.tile([P, 512], F32, tag="bank%d" % (4 + c % 2), name="xt%d" % c)
+        def spread_state(c):
+            xt = psum.tile([P, 512], F32, tag="bank6", name="xt%d" % c)
             xt3 = xt[:].rearrange("p (u m) -> p u m", u=2)
             for mt in range(M_TILES):
                 words = st_sb[mt][:, c * UNIT:(c + 1) * UNIT].bitcast(F32).rearrange("m (v u) -> m u v", u=2)
                 for u in range(2):
                     nc.tensor.transpose(out=xt3[:, u, mt * P:(mt + 1) * P], in_=words[:, u, :], identity=ident[:])
-            return xt
-
-        turned = {}
-
-        def spread_state(c, which):
-            xt = turned[c]
-            if which == 0:
-                g_a[c] = sgp.tile([P, 2048], BF16, tag="g_a", name="g_a%d" % c, align_bytes=64)
-                nc.scalar.activation(
-                    out=g_a[c][:, 0:1024].rearrange("p (m u e) -> p m u e", u=2, e=2),
-                    in_=xt[:].bitcast(BF16).rearrange("p (u m e) -> p m u e", u=2, e=2),
-                    func=ACT.Tanh,
-                )
-            else:
-                nc.scalar.copy(
-                    out=g_a[c][:, 1024:2048].bitcast(F32).rearrange("p (m u) -> p m u", u=2),
-                    in_=xt[:].rearrange("p (u m) -> p m u", u=2),
-                )
+            g_a[c] = onep.tile([P, 2048], BF16, tag="g_a", name="g_a%d" % c, align_bytes=64)
+            nc.scalar.activation(
+                out=g_a[c][:, 0:1024].rearrange("p (m u e) -> p m u e", u=2, e=2),
+                in_=xt[:].bitcast(BF16).rearrange("p (u m e) -> p m u e", u=2, e=2),
+                func=ACT.Tanh,
+            )
+            nc.scalar.copy(
+                out=g_a[c][:, 1024:2048].bitcast(F32).rearrange("p (m u) -> p m u", u=2),
+                in_=xt[:].rearrange("p (u m) -> p m u", u=2),
+            )
 
         def quant_state(c):
             cs = slice(c * 2 * M_ROWS, (c + 1) * 2 * M_ROWS)
             nc.vector.quantize_mx(out=a_codes[:, cs].bitcast(FP8X4), scales=a_scales[:, cs], in_=g_a[c][:])
             done.add(("a", c))
 
-        def tanh_rows(q):
-            for mt in range(M_TILES):
-                sl = slice(q * UNIT, (q + 1) * UNIT)
-                nc.scalar.activation(out=s32[mt][:, sl], in_=st_sb[mt][:, sl], func=ACT.Tanh)
-
-        nT = {}
-        nps = {}
-
-        def turn_noise(q):
-            nps[q] = psum.tile([P, 4, M_ROWS], BF16, tag="bank6", name="nps%d" % q)
+        def turn(tiles, nt, bank, name):
+            x = psum.tile([P, 1024], BF16, tag="bank%d" % bank, name="%s%d" % (name, nt))
             for j in range(4):
                 for mt in range(M_TILES):
                     nc.tensor.transpose(
-                        out=nps[q][:, j, mt * P:(mt + 1) * P],
-                        in_=noise_sb[mt][:, q * UNIT + j * P:q * UNIT + (j + 1) * P],
+                        out=x[:, j * M_ROWS + mt * P:j * M_ROWS + (mt + 1) * P],
+                        in_=tiles[mt][:, nt * UNIT + j * P:nt * UNIT + (j + 1) * P],
                         identity=ident_bf[:],
                     )
+            return x
 
-        def scale_noise(q):
-            nT[q] = ntp_pool.tile([P, 4, M_ROWS], F32, tag="nT", name="nT%d" % q)
-            for j in range(4):
-                nc.scalar.activation(out=nT[q][:, j, :], in_=nps[q][:, j, :], func=ACT.Copy, scale=tq[:, 4 * q + j:4 * q + j + 1])
+        s_t = {}
 
+        def tanh_columns(nt):
+            x = turn(st_sb, nt, 6, "sp")
+            s_t[nt] = twop.tile([P, 1024], F32, tag="s_t", name="s_t%d" % nt)
+            nc.scalar.activation(out=s_t[nt][:], in_=x[:], func=ACT.Tanh)
+
+        counters = {"m": 0, "q": 0, "r": 0}
         prods = {}
         grps = {}
         codes = {}
-        banks = {}
 
         def mult(u):
-            q, c, mat = unit(u)
-            raw = raws[(q, c, "W" if mat else "J")]
+            nt, c, mat = units[u]
+            tag = "W" if mat else "J"
             prod = prodp.tile([P, 4, UNIT], BF16, tag="prod", name="prod%d" % u)
-            msk = raws[(q, c, "K")]
-            parts = ((0, 256), (256, 512)) if u == 0 else ((0, 512),)
-            for lo, hi in parts:
-                nc.vector.tensor_tensor(out=prod[:, :, lo:hi], in0=raw[:, :, lo:hi], in1=msk[:, :, lo:hi], op=ALU.mult)
+            nc.vector.tensor_tensor(out=prod[:], in0=groups[(tag, nt, c)][:], in1=groups[("K", nt, c)][:], op=ALU.mult)
             prods[u] = prod
-            run_chain(1)
-            used["W" if mat else "J"] += 1
-            used["K"] += mat
+            run_chain(0 if u == 0 else 8 if u == 1 else 2)
+            for t in (tag, "K"):
+                reads_left[(t, nt, c)] -= 1
+                if reads_left[(t, nt, c)] == 0:
+                    free_bufs[t] += 1
             load_on()
 
-        def regroup_part(u, vector, lo, hi):
-            dst = grps[u][:, 4 * lo:4 * hi].rearrange("p (c i t) -> p c t i", i=4, t=4)
-            src = prods[u][:, :, lo:hi].rearrange("p t (c i) -> p c t i", i=4)
-            if vector:
+        def regroup(u):
+            grp = grpp.tile([P, 4 * UNIT], BF16, tag="grp", name="grp%d" % u, align_bytes=64)
+            dst = grp[:].rearrange("p (c i t) -> p c t i", i=8, t=4)
+            src = prods[u][:].rearrange("p t (c i) -> p c t i", i=8)
+            if u in TENSOR_REGROUPS:
+                for b in range(2):
+                    px = psum.tile([P, 1024], BF16, tag="bank%d" % (4 + b), name="px%d_%d" % (u, b))
+                    for k in range(2):
+                        lo = b * 256 + k * P
+                        nc.tensor.matmul(
+                            out=px[:, k * 512:(k + 1) * 512],
+                            lhsT=ident_bf[:],
+                            rhs=prods[u][:, :, lo:lo + P].rearrange("p t n -> p n t"),
+                            start=True,
+                            stop=True,
+                        )
+                    nc.scalar.copy(out=grp[:, b * 1024:(b + 1) * 1024], in_=px[:])
+            elif u in VECTOR_REGROUPS:
                 nc.vector.tensor_copy(out=dst, in_=src)
             else:
                 nc.scalar.copy(out=dst, in_=src)
-
-        def regroup(u):
-            grps[u] = grpp.tile([P, 4 * UNIT], BF16, tag="grp", name="grp%d" % u, align_bytes=64)
-            if u in SPLIT:
-                regroup_part(u, False, 0, SPLIT[u])
-                regroup_part(u, u > 0, SPLIT[u], UNIT)
-            else:
-                regroup_part(u, u in VECTOR_REGROUPS, 0, UNIT)
+            grps[u] = grp
+            counters["r"] = u + 1
 
         def quant(u):
-            cd = codep.tile([P, UNIT], U32, tag="codes", name="codes%d" % u, align_bytes=64)
-            sc = codep.tile([P, UNIT], U8, tag="scl", name="scl%d" % u, align_bytes=64)
+            mat = "JW"[units[u][2]]
+            cd = codep.tile([P, UNIT], U32, tag="codes" + mat, name="codes%d" % u, align_bytes=64)
+            sc = codep.tile([P, UNIT], U8, tag="scl" + mat, name="scl%d" % u, align_bytes=64)
             nc.vector.quantize_mx(out=cd[:].bitcast(FP8X4), scales=sc[:], in_=grps[u][:])
-            codes[u] = (cd, sc)
-            run_chain(1)
+            codes[units[u]] = (cd, sc)
 
-        def mx_may_go(u):
-            q, c, mat = unit(u)
-            if ("a", c) not in done:
-                return False
-            if c == 0 and q > 0:
-                return ("vec", q - 1, mat) in done
-            return True
+        BANKS = {(nt, mat): (2, 3, 4, 5) if (nt, mat) == (3, 1) else (2 * mat, 2 * mat + 1) for nt in range(4) for mat in range(2)}
+        places = {}
+        progress = {key: 0 for key in BANKS}
 
-        def mx(u):
-            q, c, mat = unit(u)
-            cd, sc = codes[u]
-            for mt in range(M_TILES):
-                idx = mat * 2 + mt
-                if c == 0:
-                    banks[idx] = psum.tile([P, UNIT], F32, tag="bank%d" % idx, name="ps%d_%d" % (q, idx))
-                lo = (2 * c + mat) * M_ROWS + mt * P
-                ms = slice(lo, lo + P)
-                nc.tensor.matmul_mx(
-                    out=banks[idx][:],
-                    lhsT=a_codes[:, ms].bitcast(FP8X4),
-                    lhsT_scale=a_scales[:, ms],
-                    rhs=cd[:].bitcast(FP8X4),
-                    rhs_scale=sc[:],
-                    start=(c == 0),
-                    stop=(c == PASSES - 1),
-                )
-            done.add(("mx", u))
+        def products(nt, mat):
+            banks = BANKS[(nt, mat)]
+            wide = len(banks) == 4
+            c0 = progress[(nt, mat)]
+            ready = c0
+            while ready < PASSES and (nt, ready, mat) in codes and ("a", ready) in done:
+                ready += 1
+            if wide and counters["r"] <= max(TENSOR_REGROUPS + (-1,)):
+                return
+            if ready == c0 or (not wide and ready < PASSES) or any(need not in done for need in NEEDS[(nt, mat)]):
+                return
+            if c0 == 0:
+                places[(nt, mat)] = [psum.tile([P, UNIT], F32, tag="bank%d" % b, name="ps%d_%d_%d" % (nt, mat, b)) for b in banks]
+            for j in range(4):
+                place = places[(nt, mat)][j if wide else j // 2]
+                lo = 0 if wide else (j % 2) * M_ROWS
+                for c in range(c0, ready):
+                    cd, sc = codes[(nt, c, mat)]
+                    ms = slice((2 * c + mat) * M_ROWS, (2 * c + mat + 1) * M_ROWS)
+                    js = slice(j * P, (j + 1) * P)
+                    nc.tensor.matmul_mx(
+                        out=place[:, lo:lo + M_ROWS],
+                        lhsT=cd[:, js].bitcast(FP8X4),
+                        lhsT_scale=sc[:, js],
+                        rhs=a_codes[:, ms].bitcast(FP8X4),
+                        rhs_scale=a_scales[:, ms],
+                        start=(c == 0),
+                        stop=(c == PASSES - 1),
+                    )
+            progress[(nt, mat)] = ready
+            if ready == PASSES:
+                done.add(("mx", nt, mat))
 
-        tmps = {}
-        xb = {}
+        NEEDS = {(nt, mat): [("F" if mat else "B", nt - 1)] if nt else [] for nt in range(4) for mat in range(2)}
+        order = [(nt, mat) for nt in range(4) for mat in range(2)]
 
-        def gain_delta(q):
-            for mt in range(M_TILES):
-                t = tmpp.tile([P, UNIT], F32, tag="t", name="t%d%d" % (mt, q))
+        def mx_catch_up():
+            for key in order:
+                if progress[key] < PASSES:
+                    products(*key)
+
+        sums = {}
+        nz = {}
+        turned = {}
+
+        def gain_delta(nt):
+            sums[nt] = twop.tile([P, 1024], F32, tag="sum", name="sum%d" % nt)
+            for b in range(2):
+                bs = slice(b * UNIT, (b + 1) * UNIT)
                 nc.vector.scalar_tensor_tensor(
-                    out=t[:], in0=banks[mt][:], scalar=lam32[:, 0:1], in1=s32[mt][:, q * UNIT:(q + 1) * UNIT],
-                    op0=ALU.mult, op1=ALU.mult,
+                    out=sums[nt][:, bs], in0=places[(nt, 0)][b][:], scalar=lam32[:, 0:1], in1=s_t[nt][:, bs], op0=ALU.mult, op1=ALU.mult
                 )
-                tmps[(mt, q)] = t
-            done.add(("vec", q, 0))
+            done.add(("B", nt))
 
-        def add_noise(q):
-            for mt in range(M_TILES):
-                t = tmps[(mt, q)]
-                nc.vector.tensor_tensor(out=t[:], in0=xb[(mt, q)][:], in1=t[:], op=ALU.add)
+        def add_noise(nt):
+            run_chain(len(chain))
+            for j in range(4):
+                js = slice(j * M_ROWS, (j + 1) * M_ROWS)
+                nc.vector.scalar_tensor_tensor(
+                    out=sums[nt][:, js], in0=nz[nt][:, js], scalar=tq[:, 4 * nt + j:4 * nt + j + 1], in1=sums[nt][:, js], op0=ALU.mult, op1=ALU.add
+                )
 
-        def add_signal(q):
-            for mt in range(M_TILES):
-                t = tmps[(mt, q)]
-                nc.vector.tensor_tensor(out=t[:], in0=banks[2 + mt][:], in1=t[:], op=ALU.add)
-            done.add(("vec", q, 1))
+        def add_signal(nt):
+            pl = places[(nt, 1)]
+            n = 1024 // len(pl)
+            for b in range(len(pl)):
+                bs = slice(b * n, (b + 1) * n)
+                nc.vector.tensor_tensor(out=sums[nt][:, bs], in0=pl[b][:, 0:n], in1=sums[nt][:, bs], op=ALU.add)
+            done.add(("D", nt))
 
-        def join(q, with_t):
+        def turn_back(nt):
             for mt in range(M_TILES):
-                x = psum.tile([P, UNIT], F32, tag="bank%d" % (7 - mt if q == SWEEPS - 1 else 4 + mt), name="x%d%d" % (mt, q))
+                o = psum.tile([P, UNIT], F32, tag="bank%d" % (mt if nt == 3 else BANKS[(nt, 1)][mt]), name="o%d%d" % (nt, mt))
                 for j in range(4):
-                    nc.tensor.matmul(out=x[:, j * P:(j + 1) * P], lhsT=nT[q][:, j, mt * P:(mt + 1) * P], rhs=ident[:], start=True, stop=not with_t)
-                    if with_t:
-                        nc.tensor.matmul(out=x[:, j * P:(j + 1) * P], lhsT=ident[:], rhs=tmps[(mt, q)][:, j * P:(j + 1) * P], start=False, stop=True)
-                xb[(mt, q)] = x
+                    nc.tensor.transpose(out=o[:, j * P:(j + 1) * P], in_=sums[nt][:, j * M_ROWS + mt * P:j * M_ROWS + (mt + 1) * P], identity=ident[:])
+                turned[(nt, mt)] = o
 
-        def finish(q):
+        def finish(nt):
             for mt in range(M_TILES):
-                t = tmps[(mt, q)]
-                src = xb[(mt, q)] if q < SWEEPS - 1 else t
-                nc.scalar.activation(out=t[:], in_=src[:], func=ACT.Tanh)
-                nc.sync.dma_start(out=out[mt * P:(mt + 1) * P, q * UNIT:(q + 1) * UNIT], in_=t[:])
+                y = outp.tile([P, UNIT], F32, tag="y", name="y%d%d" % (nt, mt))
+                nc.scalar.activation(out=y[:], in_=turned[(nt, mt)][:], func=ACT.Tanh)
+                nc.sync.dma_start(out=out[mt * P:(mt + 1) * P, nt * UNIT:(nt + 1) * UNIT], in_=y[:])
+            done.add(("F", nt))
 
-        counters = {"m": 0, "q": 0, "x": 0}
+        run_chain(CHAIN_FIRST)
 
-        def mults_to(last):
-            while counters["m"] <= min(last, UNITS - 1):
+        def mults_to(lim):
+            while counters["m"] <= min(lim, UNITS - 1):
                 mult(counters["m"])
                 counters["m"] += 1
 
-        def mx_catch_up():
-            while counters["x"] < counters["q"] and mx_may_go(counters["x"]):
-                mx(counters["x"])
-                counters["x"] += 1
-
-        def quants_to(last):
-            while counters["q"] <= min(last, UNITS - 1):
+        def quants_to(lim):
+            while counters["q"] <= min(lim, UNITS - 1):
                 quant(counters["q"])
                 counters["q"] += 1
                 mx_catch_up()
 
-        stage = [(0, 0) for w in range(SWEEPS)]
-        for i in range(UNITS + 6):
-            q, r = divmod(i, 8)
+        stage = {nt: (0, 0) for nt in range(4)}
+        for i in range(UNITS + 12):
             if i < UNITS:
                 mults_to(i)
                 regroup(i)
-            if i < 10:
-                run_chain(1)
+            for q in range(PASSES):
+                if i == ST0 + STD * q:
+                    spread_state(q)
+            for nt in range(4):
+                if i == last[(nt, 0)] - S_BEFORE:
+                    tanh_columns(nt)
             quants_to(i - QLAG)
+            for q in range(PASSES):
+                if i == ST0 + STD * q + STQ:
+                    quant_state(q)
             mx_catch_up()
-            e = i - ST0
-            if 0 <= e < 8 and e % 2 == 0:
-                turned[e // 2] = turn_state(e // 2)
-            if 1 <= e < 9:
-                spread_state((e - 1) // 2, (e - 1) % 2)
-            if 2 <= e < 10 and e % 2 == 1:
-                quant_state((e - 3) // 2)
-                mx_catch_up()
-            mults_to(i + LEAD)
-            for w in range(SWEEPS):
-                if i == (8 * w + NOISE_STEP if w else NOISE0):
-                    turn_noise(w)
-                if i == (8 * w + SCALE_STEP if w else NOISE0 + 2):
-                    scale_noise(w)
-                if i == (8 * w + TANH_STEP if w else TANH0):
-                    tanh_rows(w)
-            for w in range(SWEEPS):
-                last = w == SWEEPS - 1
-                if stage[w][0] == 0 and i >= index[(w, 0)] + 2 + DLAG and ("mx", index[(w, 0)]) in done:
-                    gain_delta(w)
-                    if last:
-                        join(w, False)
-                        add_noise(w)
-                    stage[w] = (1, i)
-                elif stage[w][0] == 1 and i > stage[w][1] and ("mx", index[(w, 1)]) in done:
-                    add_signal(w)
-                    stage[w] = (2, i)
-                    if last:
-                        finish(w)
-                elif stage[w][0] == 2 and i > stage[w][1] and not last:
-                    join(w, True)
-                    stage[w] = (3, i)
-                elif stage[w][0] == 3 and i >= stage[w][1] + FIN_LAG:
-                    finish(w)
-                    stage[w] = (4, i)
+            for nt in range(4):
+                step, at = stage[nt]
+                if step == 0 and ("mx", nt, 0) in done and i >= last[(nt, 0)] + QLAG + B_LAG:
+                    gain_delta(nt)
+                    nz[nt] = turn(noise_sb, nt, 7, "nz")
+                    stage[nt] = (1, i)
+                elif step == 1 and i >= at + A_LAG:
+                    add_noise(nt)
+                    stage[nt] = (2, i)
+                elif step == 2 and ("mx", nt, 1) in done and i >= last[(nt, 1)] + QLAG + D_LAG - (nt == 3):
+                    add_signal(nt)
+                    stage[nt] = (3, i)
+                    if nt == 3:
+                        turn_back(nt)
+                        finish(nt)
+                elif step == 3 and i >= at + O_LAG and nt < 3:
+                    turn_back(nt)
+                    stage[nt] = (4, i)
+                elif step == 4 and i >= at + F_LAG:
+                    finish(nt)
+                    stage[nt] = (5, i)
+            mults_to(i + lead(i))
             mx_catch_up()

@@ -24,30 +24,32 @@ UNITS = 32
 
 FLOPS = 2 * 2 * M_ROWS * N * N
 
-PI_HI = 3.140625
-PI_LO = math.pi - PI_HI
-SIN_COEF = (1.0, -1.0 / 6.0, 1.0 / 120.0, -1.0 / 5040.0, 1.0 / 362880.0, -1.0 / 39916800.0, 1.0 / 6227020800.0, -1.0 / 1307674368000.0)
+HALF_PI_HI = 1.5703125
+HALF_PI_LO = math.pi / 2 - HALF_PI_HI
+TERMS = [0.1 * 2.0 * (-4.0) ** k / math.factorial(2 * k + 1) for k in range(8)]
 
-VECTOR_REGROUPS = (0, 2, 6, 30)
-TENSOR_REGROUPS = (9, 13, 17, 21, 25)
+VECTOR_REGROUPS = (2, 3, 16, 24, 31)
+TENSOR_REGROUPS = (5, 9, 13)
 J_FIRST = (1, 2, 3)
 STATE_BEHIND = 5
-NOISE_BEHIND = 20
+NOISE_BEHIND = 18
 SPLIT_FIRST = 0
+BURST = 0
 LEADS = (1, 3, 2, 40, 2)
 QLAG = 2
 ST0 = 1
 STD = 2
 STQ = 2
 S_BEFORE = 2
-B_LAG = 3
+A_LAST = 2
+B_LAG = 2
 A_LAG = 2
 D_LAG = 1
 O_LAG = 1
 F_LAG = 1
 PROD_BUFS = 7
 GRP_BUFS = 5
-CODE_BUFS = 8
+CODE_BUFS = 7
 RAW_BUFS = 6
 GA_BUFS = 2
 OUT_BUFS = 2
@@ -143,44 +145,40 @@ def tile_brainquantumlayer_pb_kernel(tc, state, weights, J, theta, lam, mask, no
         th = small("th")
         k_i = small("k_i", I32)
         k_f = small("k_f")
-        x2 = small("x2")
         r1 = small("r1")
         r2 = small("r2")
         a_abs = small("a_abs")
         a_ref = small("a_ref")
         a_min = small("a_min")
         z = small("z")
-        a01 = small("a01")
         ws = {k: small("w%d" % k) for k in range(1, 8)}
         tq = small("tq")
         V = nc.vector
         th_ps = psum.tile([P, P], BF16, tag="bank7", name="th_ps")
         nc.tensor.transpose(out=th_ps[:], in_=theta_rows[:], identity=ident_bf[:])
         chain = [
-            lambda: V.tensor_copy(out=lam32[:], in_=lam_bf[:]),
             lambda: V.tensor_copy(out=th[:], in_=th_ps[:, 0:16]),
+            lambda: V.tensor_copy(out=lam32[:], in_=lam_bf[:]),
             lambda: V.tensor_scalar(out=k_i[:], in0=th[:], scalar1=2.0 / math.pi, scalar2=None, op0=ALU.mult),
             lambda: V.tensor_copy(out=k_f[:], in_=k_i[:]),
-            lambda: V.tensor_scalar(out=x2[:], in0=th[:], scalar1=2.0, scalar2=None, op0=ALU.mult),
-            lambda: V.scalar_tensor_tensor(out=r1[:], in0=k_f[:], scalar=-PI_HI, in1=x2[:], op0=ALU.mult, op1=ALU.add),
-            lambda: V.scalar_tensor_tensor(out=r2[:], in0=k_f[:], scalar=-PI_LO, in1=r1[:], op0=ALU.mult, op1=ALU.add),
+            lambda: V.scalar_tensor_tensor(out=r1[:], in0=k_f[:], scalar=-HALF_PI_HI, in1=th[:], op0=ALU.mult, op1=ALU.add),
+            lambda: V.scalar_tensor_tensor(out=r2[:], in0=k_f[:], scalar=-HALF_PI_LO, in1=r1[:], op0=ALU.mult, op1=ALU.add),
             lambda: V.scalar_tensor_tensor(out=a_abs[:], in0=r2[:], scalar=-1.0, in1=r2[:], op0=ALU.mult, op1=ALU.max),
-            lambda: V.tensor_scalar(out=a_ref[:], in0=a_abs[:], scalar1=-1.0, scalar2=math.pi, op0=ALU.mult, op1=ALU.add),
+            lambda: V.tensor_scalar(out=a_ref[:], in0=a_abs[:], scalar1=-1.0, scalar2=math.pi / 2, op0=ALU.mult, op1=ALU.add),
             lambda: V.tensor_tensor(out=a_min[:], in0=a_abs[:], in1=a_ref[:], op=ALU.min),
             lambda: V.tensor_tensor(out=z[:], in0=a_min[:], in1=a_min[:], op=ALU.mult),
-            lambda: V.tensor_scalar(out=a01[:], in0=a_min[:], scalar1=0.1, scalar2=None, op0=ALU.mult),
-            lambda: V.tensor_scalar(out=ws[7][:], in0=z[:], scalar1=SIN_COEF[7], scalar2=None, op0=ALU.mult),
+            lambda: V.tensor_scalar(out=ws[7][:], in0=z[:], scalar1=TERMS[7], scalar2=None, op0=ALU.mult),
         ]
 
         def horner(k):
             return lambda: V.scalar_tensor_tensor(
-                out=ws[k][:], in0=ws[k + 1][:], scalar=SIN_COEF[k], in1=z[:], op0=ALU.add, op1=ALU.mult
+                out=ws[k][:], in0=ws[k + 1][:], scalar=TERMS[k], in1=z[:], op0=ALU.add, op1=ALU.mult
             )
 
         for k in range(6, 0, -1):
             chain.append(horner(k))
         chain.append(
-            lambda: V.scalar_tensor_tensor(out=tq[:], in0=ws[1][:], scalar=1.0, in1=a01[:], op0=ALU.add, op1=ALU.mult)
+            lambda: V.scalar_tensor_tensor(out=tq[:], in0=ws[1][:], scalar=TERMS[0], in1=a_min[:], op0=ALU.add, op1=ALU.mult)
         )
         chain_pos = {"n": 0}
 
@@ -287,25 +285,28 @@ def tile_brainquantumlayer_pb_kernel(tc, state, weights, J, theta, lam, mask, no
 
         BANKS = {(nt, mat): (2, 3, 4, 5) if (nt, mat) == (3, 1) else (2 * mat, 2 * mat + 1) for nt in range(4) for mat in range(2)}
         places = {}
-        progress = {key: 0 for key in BANKS}
+        progress = {(nt, mat, j): 0 for nt, mat in BANKS for j in range(4)}
 
         def products(nt, mat):
             banks = BANKS[(nt, mat)]
             wide = len(banks) == 4
-            c0 = progress[(nt, mat)]
-            ready = c0
-            while ready < PASSES and (nt, ready, mat) in codes and ("a", ready) in done:
-                ready += 1
             if wide and counters["r"] <= max(TENSOR_REGROUPS + (-1,)):
                 return
-            if ready == c0 or (not wide and ready < PASSES) or any(need not in done for need in NEEDS[(nt, mat)]):
+            if any(need not in done for need in NEEDS[(nt, mat)]):
                 return
-            if c0 == 0:
+            ready = 0
+            while ready < PASSES and (nt, ready, mat) in codes and ("a", ready) in done:
+                ready += 1
+            if ready == 0 or (BURST and not wide and ready < PASSES):
+                return
+            if (nt, mat) not in places:
                 places[(nt, mat)] = [psum.tile([P, UNIT], F32, tag="bank%d" % b, name="ps%d_%d_%d" % (nt, mat, b)) for b in banks]
-            for j in range(4):
+            for j in (0, 1, 2, 3) if wide else (0, 2, 1, 3):
                 place = places[(nt, mat)][j if wide else j // 2]
                 lo = 0 if wide else (j % 2) * M_ROWS
-                for c in range(c0, ready):
+                if not wide and j % 2 == 1 and ready < PASSES:
+                    continue
+                for c in range(progress[(nt, mat, j)], ready):
                     cd, sc = codes[(nt, c, mat)]
                     ms = slice((2 * c + mat) * M_ROWS, (2 * c + mat + 1) * M_ROWS)
                     js = slice(j * P, (j + 1) * P)
@@ -318,7 +319,7 @@ def tile_brainquantumlayer_pb_kernel(tc, state, weights, J, theta, lam, mask, no
                         start=(c == 0),
                         stop=(c == PASSES - 1),
                     )
-            progress[(nt, mat)] = ready
+                progress[(nt, mat, j)] = ready
             if ready == PASSES:
                 done.add(("mx", nt, mat))
 
@@ -327,7 +328,7 @@ def tile_brainquantumlayer_pb_kernel(tc, state, weights, J, theta, lam, mask, no
 
         def mx_catch_up():
             for key in order:
-                if progress[key] < PASSES:
+                if ("mx",) + key not in done:
                     products(*key)
 
         sums = {}
@@ -361,7 +362,7 @@ def tile_brainquantumlayer_pb_kernel(tc, state, weights, J, theta, lam, mask, no
 
         def turn_back(nt):
             for mt in range(M_TILES):
-                o = psum.tile([P, UNIT], F32, tag="bank%d" % (mt if nt == 3 else BANKS[(nt, 1)][mt]), name="o%d%d" % (nt, mt))
+                o = psum.tile([P, UNIT], F32, tag="bank%d" % BANKS[(nt, 1)][mt], name="o%d%d" % (nt, mt))
                 for j in range(4):
                     nc.tensor.transpose(out=o[:, j * P:(j + 1) * P], in_=sums[nt][:, j * M_ROWS + mt * P:j * M_ROWS + (mt + 1) * P], identity=ident[:])
                 turned[(nt, mt)] = o
@@ -372,6 +373,20 @@ def tile_brainquantumlayer_pb_kernel(tc, state, weights, J, theta, lam, mask, no
                 nc.scalar.activation(out=y[:], in_=turned[(nt, mt)][:], func=ACT.Tanh)
                 nc.sync.dma_start(out=out[mt * P:(mt + 1) * P, nt * UNIT:(nt + 1) * UNIT], in_=y[:])
             done.add(("F", nt))
+
+        def finish_last(nt):
+            ys = [outp.tile([P, UNIT], F32, tag="y", name="y%d%d" % (nt, mt)) for mt in range(M_TILES)]
+            for half in range(2):
+                obanks = [psum.tile([P, UNIT], F32, tag="bank%d" % ((0, 1, 6, 7)[2 * half + mt]), name="o%d%d%d" % (nt, mt, half)) for mt in range(M_TILES)]
+                for jj in range(2):
+                    j = 2 * half + jj
+                    for mt in range(M_TILES):
+                        nc.tensor.transpose(out=obanks[mt][:, jj * P:(jj + 1) * P], in_=sums[nt][:, j * M_ROWS + mt * P:j * M_ROWS + (mt + 1) * P], identity=ident[:])
+                for mt in range(M_TILES):
+                    hs = slice(half * M_ROWS, (half + 1) * M_ROWS)
+                    nc.scalar.activation(out=ys[mt][:, hs], in_=obanks[mt][:, 0:M_ROWS], func=ACT.Tanh)
+                    col = nt * UNIT + half * M_ROWS
+                    nc.sync.dma_start(out=out[mt * P:(mt + 1) * P, col:col + M_ROWS], in_=ys[mt][:, hs])
 
         run_chain(CHAIN_FIRST)
 
@@ -408,15 +423,14 @@ def tile_brainquantumlayer_pb_kernel(tc, state, weights, J, theta, lam, mask, no
                     gain_delta(nt)
                     nz[nt] = turn(noise_sb, nt, 7, "nz")
                     stage[nt] = (1, i)
-                elif step == 1 and i >= at + A_LAG:
+                elif step == 1 and i >= at + (A_LAG if nt < 3 else A_LAST):
                     add_noise(nt)
                     stage[nt] = (2, i)
                 elif step == 2 and ("mx", nt, 1) in done and i >= last[(nt, 1)] + QLAG + D_LAG - (nt == 3):
                     add_signal(nt)
                     stage[nt] = (3, i)
                     if nt == 3:
-                        turn_back(nt)
-                        finish(nt)
+                        finish_last(nt)
                 elif step == 3 and i >= at + O_LAG and nt < 3:
                     turn_back(nt)
                     stage[nt] = (4, i)

@@ -28,31 +28,34 @@ HALF_PI_HI = 1.5703125
 HALF_PI_LO = math.pi / 2 - HALF_PI_HI
 TERMS = [0.1 * 2.0 * (-4.0) ** k / math.factorial(2 * k + 1) for k in range(8)]
 
-VECTOR_REGROUPS = (2, 3, 16, 24, 31)
-TENSOR_REGROUPS = (5, 9, 13)
-J_FIRST = (1, 2, 3)
-STATE_BEHIND = 5
-NOISE_BEHIND = 18
-SPLIT_FIRST = 0
-BURST = 0
-LEADS = (1, 3, 2, 40, 2)
+VECTOR_REGROUPS = (2, 6, 22, 30)
+TENSOR_REGROUPS = (9, 10, 11, 12, 13, 14)
+TILE_MAJOR = (1,)
+J_FIRST = (3,)
+PAIRS = ()
+LOADS = "ABC"
+STATE_BEHIND = 1
+NOISE_BEHIND = 3
+LEADS = (1, 3, 2, 12, 3)
 QLAG = 2
-ST0 = 1
+ST0 = 4
 STD = 2
 STQ = 2
-S_BEFORE = 2
-A_LAST = 2
-B_LAG = 2
+S_BEFORE = 1
+A_LAST = 1
+B_LAG = 3
 A_LAG = 2
-D_LAG = 1
+D_LAG = 3
 O_LAG = 1
-F_LAG = 1
+F_LAG = 2
 PROD_BUFS = 7
-GRP_BUFS = 5
-CODE_BUFS = 7
-RAW_BUFS = 6
+GRP_BUFS = 4
+CODE_BUFS = 9
+RAW_BUFS = 3
+G0 = 0
+BUFS = {"J": RAW_BUFS, "K": RAW_BUFS + 1, "W": RAW_BUFS}
 GA_BUFS = 2
-OUT_BUFS = 2
+OUT_BUFS = 4
 CHAIN_FIRST = 0
 
 
@@ -75,11 +78,20 @@ def tile_brainquantumlayer_pb_kernel(tc, state, weights, J, theta, lam, mask, no
         ctx.enter_context(tc.manual_schedule())
 
         units = []
-        for nt in range(4):
-            if nt in J_FIRST:
-                units += [(nt, c, mat) for mat in range(2) for c in range(PASSES)]
+        for h in range(2):
+            if h in TILE_MAJOR:
+                for nt in (2 * h, 2 * h + 1):
+                    if nt in J_FIRST:
+                        units += [(nt, c, mat) for mat in range(2) for c in range(PASSES)]
+                    else:
+                        units += [(nt, c, mat) for c in range(PASSES) for mat in range(2)]
             else:
-                units += [(nt, c, mat) for c in range(PASSES) for mat in range(2)]
+                for c in range(PASSES):
+                    g = h * PASSES + c
+                    if g in PAIRS:
+                        units += [(2 * h + k, cc, mat) for mat in range(2) for cc in (c, c + 1) for k in range(2)]
+                    elif g - 1 not in PAIRS:
+                        units += [(2 * h + k, c, mat) for k, mat in (((0, 0), (0, 1), (1, 0), (1, 1)) if g == 0 and G0 else ((0, 0), (1, 0), (0, 1), (1, 1)))]
         last = {(nt, mat): max(u for u in range(UNITS) if units[u][0] == nt and units[u][2] == mat) for nt in range(4) for mat in range(2)}
 
         theta_rows = const.tile([P, P], BF16, name="theta_rows")
@@ -101,40 +113,61 @@ def tile_brainquantumlayer_pb_kernel(tc, state, weights, J, theta, lam, mask, no
             for mt in range(M_TILES):
                 nc.sync.dma_start(out=tiles[mt][:], in_=source[mt * P:(mt + 1) * P, :])
 
-        loads = []
-        for nt in range(4):
-            if nt in J_FIRST:
-                part = [(tag, nt, c) for c in range(PASSES) for tag in ("J", "K")] + [("W", nt, c) for c in range(PASSES)]
-            else:
-                part = [(tag, nt, c) for c in range(PASSES) for tag in ("J", "K", "W")]
-            for item in part:
-                loads.append(item)
-                if len(loads) == STATE_BEHIND:
-                    loads.append(("S", 0, 0))
-                if len(loads) == NOISE_BEHIND:
-                    loads.append(("N", 0, 0))
-        free_bufs = {"J": RAW_BUFS, "K": RAW_BUFS, "W": RAW_BUFS}
+        first = {"a": ("J", 0, UNIT), "b": ("K", 0, UNIT), "c": ("W", 0, UNIT), "d": ("J", UNIT, HALF), "e": ("K", UNIT, HALF), "f": ("W", UNIT, HALF),
+                 "A": ("J", 0, HALF), "B": ("K", 0, HALF), "C": ("W", 0, HALF)}
+        loads = list(LOADS)
+        for g in range(1, PASSES if 1 in TILE_MAJOR else 2 * PASSES):
+            if g in PAIRS:
+                loads += [(tag, k) for k in (g, g + 1) for tag in ("J", "K")] + [("W", g), ("W", g + 1)]
+            elif g - 1 not in PAIRS:
+                loads += [(tag, g) for tag in ("J", "K", "W")]
+            if g == STATE_BEHIND:
+                loads.append("S")
+            if g == NOISE_BEHIND:
+                loads.append("N")
+        if 1 in TILE_MAJOR:
+            for nt in (2, 3):
+                if nt in J_FIRST:
+                    loads += [(tag, nt, c) for c in range(PASSES) for tag in ("J", "K")] + [("W", nt, c) for c in range(PASSES)]
+                else:
+                    loads += [(tag, nt, c) for c in range(PASSES) for tag in ("J", "K", "W")]
+        free_bufs = dict(BUFS)
         reads_left = {}
+
+        def load_piece(g, tag, lo, hi):
+            if (tag, g) not in groups:
+                free_bufs[tag] -= 1
+                reads_left[(tag, g)] = 4 if tag == "K" else 2
+                groups[(tag, g)] = rawp.tile([P, 4, HALF], BF16, tag=tag, name="raw%s%d" % (tag, g), bufs=BUFS[tag])
+            h, c = divmod(g, PASSES)
+            src = sources[tag][c * UNIT:(c + 1) * UNIT, h * HALF + lo:h * HALF + hi]
+            nc.sync.dma_start(out=groups[(tag, g)][:, :, lo:hi], in_=src.rearrange("(p j) w -> p j w", j=4))
 
         def load_on():
             while loads:
-                tag, nt, c = loads[0]
-                if tag == "S":
+                item = loads[0]
+                if item == "S":
                     load_rows(st_sb, state)
-                elif tag == "N":
+                elif item == "N":
                     load_rows(noise_sb, noise_raw)
-                else:
+                elif item in first:
+                    tag, lo, hi = first[item]
+                    load_piece(0, tag, lo, hi)
+                elif len(item) == 3:
+                    tag, nt, c = item
                     if free_bufs[tag] == 0:
                         return
                     free_bufs[tag] -= 1
-                    reads_left[(tag, nt, c)] = 2 if tag == "K" else 1
-                    raw = rawp.tile([P, 4, UNIT], BF16, tag=tag, name="raw%s%d%d" % (tag, nt, c))
-                    groups[(tag, nt, c)] = raw
+                    reads_left[item] = 2 if tag == "K" else 1
+                    groups[item] = rawp.tile([P, 4, UNIT], BF16, tag=tag, name="raw%s%d%d" % (tag, nt, c), bufs=BUFS[tag])
                     src = sources[tag][c * UNIT:(c + 1) * UNIT, nt * UNIT:(nt + 1) * UNIT]
-                    cuts = (0, 256, 512) if SPLIT_FIRST and (nt, c) == (0, 0) and tag != "W" else (0, 512)
-                    for lo, hi in zip(cuts, cuts[1:]):
-                        nc.sync.dma_start(out=raw[:, :, lo:hi], in_=src.rearrange("(p j) w -> p j w", j=4)[:, :, lo:hi])
-                loads.remove(loads[0])
+                    nc.sync.dma_start(out=groups[item][:], in_=src.rearrange("(p j) w -> p j w", j=4))
+                else:
+                    tag, g = item
+                    if free_bufs[tag] == 0:
+                        return
+                    load_piece(g, tag, 0, HALF)
+                loads.remove(item)
 
         load_on()
 
@@ -243,12 +276,19 @@ def tile_brainquantumlayer_pb_kernel(tc, state, weights, J, theta, lam, mask, no
             nt, c, mat = units[u]
             tag = "W" if mat else "J"
             prod = prodp.tile([P, 4, UNIT], BF16, tag="prod", name="prod%d" % u)
-            nc.vector.tensor_tensor(out=prod[:], in0=groups[(tag, nt, c)][:], in1=groups[("K", nt, c)][:], op=ALU.mult)
+            h, k = divmod(nt, 2)
+            if h in TILE_MAJOR:
+                keys = {t: (t, nt, c) for t in (tag, "K")}
+                views = [groups[keys[t]][:] for t in (tag, "K")]
+            else:
+                keys = {t: (t, h * PASSES + c) for t in (tag, "K")}
+                views = [groups[keys[t]][:, :, k * UNIT:(k + 1) * UNIT] for t in (tag, "K")]
+            nc.vector.tensor_tensor(out=prod[:], in0=views[0], in1=views[1], op=ALU.mult)
             prods[u] = prod
             run_chain(0 if u == 0 else 8 if u == 1 else 2)
             for t in (tag, "K"):
-                reads_left[(t, nt, c)] -= 1
-                if reads_left[(t, nt, c)] == 0:
+                reads_left[keys[t]] -= 1
+                if reads_left[keys[t]] == 0:
                     free_bufs[t] += 1
             load_on()
 
@@ -283,7 +323,7 @@ def tile_brainquantumlayer_pb_kernel(tc, state, weights, J, theta, lam, mask, no
             nc.vector.quantize_mx(out=cd[:].bitcast(FP8X4), scales=sc[:], in_=grps[u][:])
             codes[units[u]] = (cd, sc)
 
-        BANKS = {(nt, mat): (2, 3, 4, 5) if (nt, mat) == (3, 1) else (2 * mat, 2 * mat + 1) for nt in range(4) for mat in range(2)}
+        BANKS = {(nt, mat): (2, 3, 4, 5) if (nt, mat) == (3, 1) else ((0, 1), (2, 3))[nt % 2] for nt in range(4) for mat in range(2)}
         places = {}
         progress = {(nt, mat, j): 0 for nt, mat in BANKS for j in range(4)}
 
@@ -297,15 +337,13 @@ def tile_brainquantumlayer_pb_kernel(tc, state, weights, J, theta, lam, mask, no
             ready = 0
             while ready < PASSES and (nt, ready, mat) in codes and ("a", ready) in done:
                 ready += 1
-            if ready == 0 or (BURST and not wide and ready < PASSES):
+            if ready == 0 or (not wide and ready < PASSES):
                 return
             if (nt, mat) not in places:
                 places[(nt, mat)] = [psum.tile([P, UNIT], F32, tag="bank%d" % b, name="ps%d_%d_%d" % (nt, mat, b)) for b in banks]
-            for j in (0, 1, 2, 3) if wide else (0, 2, 1, 3):
+            for j in range(4):
                 place = places[(nt, mat)][j if wide else j // 2]
                 lo = 0 if wide else (j % 2) * M_ROWS
-                if not wide and j % 2 == 1 and ready < PASSES:
-                    continue
                 for c in range(progress[(nt, mat, j)], ready):
                     cd, sc = codes[(nt, c, mat)]
                     ms = slice((2 * c + mat) * M_ROWS, (2 * c + mat + 1) * M_ROWS)
@@ -323,8 +361,8 @@ def tile_brainquantumlayer_pb_kernel(tc, state, weights, J, theta, lam, mask, no
             if ready == PASSES:
                 done.add(("mx", nt, mat))
 
-        NEEDS = {(nt, mat): [("F" if mat else "B", nt - 1)] if nt else [] for nt in range(4) for mat in range(2)}
-        order = [(nt, mat) for nt in range(4) for mat in range(2)]
+        NEEDS = {(nt, mat): [("B", nt)] if mat else [("F", nt - 2)] if nt > 1 else [] for nt in range(4) for mat in range(2)}
+        order = [(nt, mat) for h in range(2) for mat in range(2) for nt in (2 * h, 2 * h + 1)]
 
         def mx_catch_up():
             for key in order:
@@ -351,6 +389,7 @@ def tile_brainquantumlayer_pb_kernel(tc, state, weights, J, theta, lam, mask, no
                 nc.vector.scalar_tensor_tensor(
                     out=sums[nt][:, js], in0=nz[nt][:, js], scalar=tq[:, 4 * nt + j:4 * nt + j + 1], in1=sums[nt][:, js], op0=ALU.mult, op1=ALU.add
                 )
+            done.add(("A", nt))
 
         def add_signal(nt):
             pl = places[(nt, 1)]
@@ -419,18 +458,22 @@ def tile_brainquantumlayer_pb_kernel(tc, state, weights, J, theta, lam, mask, no
             mx_catch_up()
             for nt in range(4):
                 step, at = stage[nt]
-                if step == 0 and ("mx", nt, 0) in done and i >= last[(nt, 0)] + QLAG + B_LAG:
+                if step == 0 and ("mx", nt, 0) in done and (nt == 0 or ("A", nt - 1) in done) and i >= last[(nt, 0)] + QLAG + B_LAG:
                     gain_delta(nt)
                     nz[nt] = turn(noise_sb, nt, 7, "nz")
                     stage[nt] = (1, i)
                 elif step == 1 and i >= at + (A_LAG if nt < 3 else A_LAST):
                     add_noise(nt)
                     stage[nt] = (2, i)
-                elif step == 2 and ("mx", nt, 1) in done and i >= last[(nt, 1)] + QLAG + D_LAG - (nt == 3):
+                elif step == 2 and ("mx", nt, 1) in done and i >= last[(nt, 1)] + QLAG + (0 if last[(nt, 1)] >= UNITS - 2 else D_LAG):
                     add_signal(nt)
                     stage[nt] = (3, i)
                     if nt == 3:
                         finish_last(nt)
+                    elif nt == 2 and 1 not in TILE_MAJOR:
+                        turn_back(nt)
+                        finish(nt)
+                        stage[nt] = (5, i)
                 elif step == 3 and i >= at + O_LAG and nt < 3:
                     turn_back(nt)
                     stage[nt] = (4, i)

@@ -28,26 +28,26 @@ HALF_PI_HI = 1.5703125
 HALF_PI_LO = math.pi / 2 - HALF_PI_HI
 TERMS = [0.1 * 2.0 * (-4.0) ** k / math.factorial(2 * k + 1) for k in range(8)]
 
-VECTOR_REGROUPS = (2, 6, 22, 30)
-TENSOR_REGROUPS = (9, 10, 11, 12, 13, 14)
+VECTOR_REGROUPS = (2, 6, 10, 14, 22, 30)
+TENSOR_REGROUPS = ()
 TILE_MAJOR = (1,)
 J_FIRST = (3,)
 PAIRS = ()
 LOADS = "ABC"
-STATE_BEHIND = 1
+STATE_PLAN = ((0, 1), (2, 3), (), ())
 NOISE_BEHIND = 3
-LEADS = (1, 3, 2, 12, 3)
+LEADS = (1, 3, 2, 7, 3)
 QLAG = 2
-ST0 = 4
+ST0 = 1
 STD = 2
 STQ = 2
 S_BEFORE = 1
-A_LAST = 1
+A_LAST = 0
 B_LAG = 3
-A_LAG = 2
-D_LAG = 3
+A_LAG = 0
+D_LAG = 1
 O_LAG = 1
-F_LAG = 2
+F_LAG = 1
 PROD_BUFS = 7
 GRP_BUFS = 4
 CODE_BUFS = 9
@@ -115,14 +115,13 @@ def tile_brainquantumlayer_pb_kernel(tc, state, weights, J, theta, lam, mask, no
 
         first = {"a": ("J", 0, UNIT), "b": ("K", 0, UNIT), "c": ("W", 0, UNIT), "d": ("J", UNIT, HALF), "e": ("K", UNIT, HALF), "f": ("W", UNIT, HALF),
                  "A": ("J", 0, HALF), "B": ("K", 0, HALF), "C": ("W", 0, HALF)}
-        loads = list(LOADS)
+        loads = list(LOADS) + ["s%d" % c for c in STATE_PLAN[0]]
         for g in range(1, PASSES if 1 in TILE_MAJOR else 2 * PASSES):
             if g in PAIRS:
                 loads += [(tag, k) for k in (g, g + 1) for tag in ("J", "K")] + [("W", g), ("W", g + 1)]
             elif g - 1 not in PAIRS:
                 loads += [(tag, g) for tag in ("J", "K", "W")]
-            if g == STATE_BEHIND:
-                loads.append("S")
+            loads += ["s%d" % c for c in STATE_PLAN[g]]
             if g == NOISE_BEHIND:
                 loads.append("N")
         if 1 in TILE_MAJOR:
@@ -146,8 +145,10 @@ def tile_brainquantumlayer_pb_kernel(tc, state, weights, J, theta, lam, mask, no
         def load_on():
             while loads:
                 item = loads[0]
-                if item == "S":
-                    load_rows(st_sb, state)
+                if item[0] == "s":
+                    c = int(item[1])
+                    for mt in range(M_TILES):
+                        nc.sync.dma_start(out=st_sb[mt][:, c * UNIT:(c + 1) * UNIT], in_=state[mt * P:(mt + 1) * P, c * UNIT:(c + 1) * UNIT])
                 elif item == "N":
                     load_rows(noise_sb, noise_raw)
                 elif item in first:
@@ -191,7 +192,6 @@ def tile_brainquantumlayer_pb_kernel(tc, state, weights, J, theta, lam, mask, no
         nc.tensor.transpose(out=th_ps[:], in_=theta_rows[:], identity=ident_bf[:])
         chain = [
             lambda: V.tensor_copy(out=th[:], in_=th_ps[:, 0:16]),
-            lambda: V.tensor_copy(out=lam32[:], in_=lam_bf[:]),
             lambda: V.tensor_scalar(out=k_i[:], in0=th[:], scalar1=2.0 / math.pi, scalar2=None, op0=ALU.mult),
             lambda: V.tensor_copy(out=k_f[:], in_=k_i[:]),
             lambda: V.scalar_tensor_tensor(out=r1[:], in0=k_f[:], scalar=-HALF_PI_HI, in1=th[:], op0=ALU.mult, op1=ALU.add),
@@ -213,6 +213,7 @@ def tile_brainquantumlayer_pb_kernel(tc, state, weights, J, theta, lam, mask, no
         chain.append(
             lambda: V.scalar_tensor_tensor(out=tq[:], in0=ws[1][:], scalar=TERMS[0], in1=a_min[:], op0=ALU.add, op1=ALU.mult)
         )
+        chain.append(lambda: V.tensor_copy(out=lam32[:], in_=lam_bf[:]))
         chain_pos = {"n": 0}
 
         def run_chain(count):
@@ -299,12 +300,11 @@ def tile_brainquantumlayer_pb_kernel(tc, state, weights, J, theta, lam, mask, no
             if u in TENSOR_REGROUPS:
                 for b in range(2):
                     px = psum.tile([P, 1024], BF16, tag="bank%d" % (4 + b), name="px%d_%d" % (u, b))
-                    for k in range(2):
-                        lo = b * 256 + k * P
+                    for t in range(4):
                         nc.tensor.matmul(
-                            out=px[:, k * 512:(k + 1) * 512],
+                            out=px[:].rearrange("p (n t) -> p n t", t=4)[:, :, t],
                             lhsT=ident_bf[:],
-                            rhs=prods[u][:, :, lo:lo + P].rearrange("p t n -> p n t"),
+                            rhs=prods[u][:, t, b * 256:(b + 1) * 256],
                             start=True,
                             stop=True,
                         )

@@ -28,31 +28,31 @@ HALF_PI_HI = 1.5703125
 HALF_PI_LO = math.pi / 2 - HALF_PI_HI
 TERMS = [0.1 * 2.0 * (-4.0) ** k / math.factorial(2 * k + 1) for k in range(8)]
 
-VECTOR_REGROUPS = (2, 6, 10, 14, 22, 30)
+VECTOR_REGROUPS = (3, 5, 11, 23, 29)
 TENSOR_REGROUPS = ()
 TILE_MAJOR = (1,)
 J_FIRST = (3,)
-PAIRS = ()
-LOADS = "ABC"
+PAIRS = (2,)
+LOADS = "abCde"
 STATE_PLAN = ((0, 1), (2, 3), (), ())
 NOISE_BEHIND = 3
-LEADS = (1, 3, 2, 7, 3)
-QLAG = 2
-ST0 = 1
-STD = 2
-STQ = 2
+LEADS = (1, 3, 2, 7, 4)
+QLAG = 1
+ST0 = 2
+STD = 1
+STQ = 1
 S_BEFORE = 1
-A_LAST = 0
+A_LAST = 2
 B_LAG = 3
-A_LAG = 0
-D_LAG = 1
+A_LAG = 2
+D_LAG = 2
 O_LAG = 1
 F_LAG = 1
 PROD_BUFS = 7
-GRP_BUFS = 4
+GRP_BUFS = 5
 CODE_BUFS = 9
 RAW_BUFS = 3
-G0 = 0
+G0 = 1
 BUFS = {"J": RAW_BUFS, "K": RAW_BUFS + 1, "W": RAW_BUFS}
 GA_BUFS = 2
 OUT_BUFS = 4

import math
from contextlib import ExitStack

import concourse.mybir as mybir
from concourse.masks import make_identity

FP8X4 = mybir.dt.float8_e4m3fn_x4
BF16 = mybir.dt.bfloat16
F32 = mybir.dt.float32
I32 = mybir.dt.int32
U32 = mybir.dt.uint32
U8 = mybir.dt.uint8
ALU = mybir.AluOpType
ACT = mybir.ActivationFunctionType

P = 128
M_ROWS = 256
N = 2048
M_TILES = 2
PASSES = 4
HALF = 1024
UNIT = 512
UNITS = 32

FLOPS = 2 * 2 * M_ROWS * N * N

HALF_PI_HI = 1.5703125
HALF_PI_LO = math.pi / 2 - HALF_PI_HI
TERMS = [0.1 * 2.0 * (-4.0) ** k / math.factorial(2 * k + 1) for k in range(8)]

VECTOR_REGROUPS = (3, 5, 11, 23, 29)
TENSOR_REGROUPS = ()
TILE_MAJOR = (1,)
J_FIRST = (3,)
PAIRS = (2,)
LOADS = "abCde"
STATE_PLAN = ((0, 1), (2, 3), (), ())
NOISE_BEHIND = 3
LEADS = (1, 3, 2, 7, 4)
QLAG = 1
ST0 = 2
STD = 1
STQ = 1
S_BEFORE = 1
A_LAST = 2
B_LAG = 3
A_LAG = 2
D_LAG = 2
O_LAG = 1
F_LAG = 1
PROD_BUFS = 7
GRP_BUFS = 5
CODE_BUFS = 9
RAW_BUFS = 3
G0 = 1
BUFS = {"J": RAW_BUFS, "K": RAW_BUFS + 1, "W": RAW_BUFS}
GA_BUFS = 2
OUT_BUFS = 4
CHAIN_FIRST = 0


def lead(i):
    return LEADS[0] if i < LEADS[1] else (LEADS[2] if i < LEADS[3] else LEADS[4])


def tile_brainquantumlayer_pb_kernel(tc, state, weights, J, theta, lam, mask, noise_raw, out):
    nc = tc.nc
    with ExitStack() as ctx:
        const = ctx.enter_context(tc.tile_pool(name="const", bufs=1))
        rawp = ctx.enter_context(tc.tile_pool(name="raw", bufs=RAW_BUFS))
        prodp = ctx.enter_context(tc.tile_pool(name="prod", bufs=PROD_BUFS))
        grpp = ctx.enter_context(tc.tile_pool(name="grp", bufs=GRP_BUFS))
        codep = ctx.enter_context(tc.tile_pool(name="code", bufs=CODE_BUFS))
        twop = ctx.enter_context(tc.tile_pool(name="two", bufs=2))
        onep = ctx.enter_context(tc.tile_pool(name="one", bufs=GA_BUFS))
        outp = ctx.enter_context(tc.tile_pool(name="outp", bufs=OUT_BUFS))
        psum = ctx.enter_context(tc.psum_pool(name="psum", bufs=1))
        ctx.enter_context(tc.manual_schedule())

        units = []
        for h in range(2):
            if h in TILE_MAJOR:
                for nt in (2 * h, 2 * h + 1):
                    if nt in J_FIRST:
                        units += [(nt, c, mat) for mat in range(2) for c in range(PASSES)]
                    else:
                        units += [(nt, c, mat) for c in range(PASSES) for mat in range(2)]
            else:
                for c in range(PASSES):
                    g = h * PASSES + c
                    if g in PAIRS:
                        units += [(2 * h + k, cc, mat) for mat in range(2) for cc in (c, c + 1) for k in range(2)]
                    elif g - 1 not in PAIRS:
                        units += [(2 * h + k, c, mat) for k, mat in (((0, 0), (0, 1), (1, 0), (1, 1)) if g == 0 and G0 else ((0, 0), (1, 0), (0, 1), (1, 1)))]
        last = {(nt, mat): max(u for u in range(UNITS) if units[u][0] == nt and units[u][2] == mat) for nt in range(4) for mat in range(2)}

        theta_rows = const.tile([P, P], BF16, name="theta_rows")
        nc.gpsimd.memset(theta_rows[:], 0.0)
        ident = const.tile([P, P], F32, name="ident")
        make_identity(nc, ident[:])
        ident_bf = const.tile([P, P], BF16, name="ident_bf")
        nc.gpsimd.tensor_copy(out=ident_bf[:], in_=ident[:])
        nc.scalar.dma_start(out=theta_rows[0:16, :], in_=theta.rearrange("(b p) -> b p", b=16))
        lam_bf = const.tile([P, 1], BF16, name="lam_bf")
        nc.scalar.dma_start(out=lam_bf[:], in_=lam.partition_broadcast(P))

        sources = {"J": J, "K": mask, "W": weights}
        groups = {}
        st_sb = [const.tile([P, N], BF16, name="st%d" % mt) for mt in range(M_TILES)]
        noise_sb = [const.tile([P, N], BF16, name="noise%d" % mt) for mt in range(M_TILES)]

        def load_rows(tiles, source):
            for mt in range(M_TILES):
                nc.sync.dma_start(out=tiles[mt][:], in_=source[mt * P:(mt + 1) * P, :])

        first = {"a": ("J", 0, UNIT), "b": ("K", 0, UNIT), "c": ("W", 0, UNIT), "d": ("J", UNIT, HALF), "e": ("K", UNIT, HALF), "f": ("W", UNIT, HALF),
                 "A": ("J", 0, HALF), "B": ("K", 0, HALF), "C": ("W", 0, HALF)}
        loads = list(LOADS) + ["s%d" % c for c in STATE_PLAN[0]]
        for g in range(1, PASSES if 1 in TILE_MAJOR else 2 * PASSES):
            if g in PAIRS:
                loads += [(tag, k) for k in (g, g + 1) for tag in ("J", "K")] + [("W", g), ("W", g + 1)]
            elif g - 1 not in PAIRS:
                loads += [(tag, g) for tag in ("J", "K", "W")]
            loads += ["s%d" % c for c in STATE_PLAN[g]]
            if g == NOISE_BEHIND:
                loads.append("N")
        if 1 in TILE_MAJOR:
            for nt in (2, 3):
                if nt in J_FIRST:
                    loads += [(tag, nt, c) for c in range(PASSES) for tag in ("J", "K")] + [("W", nt, c) for c in range(PASSES)]
                else:
                    loads += [(tag, nt, c) for c in range(PASSES) for tag in ("J", "K", "W")]
        free_bufs = dict(BUFS)
        reads_left = {}

        def load_piece(g, tag, lo, hi):
            if (tag, g) not in groups:
                free_bufs[tag] -= 1
                reads_left[(tag, g)] = 4 if tag == "K" else 2
                groups[(tag, g)] = rawp.tile([P, 4, HALF], BF16, tag=tag, name="raw%s%d" % (tag, g), bufs=BUFS[tag])
            h, c = divmod(g, PASSES)
            src = sources[tag][c * UNIT:(c + 1) * UNIT, h * HALF + lo:h * HALF + hi]
            nc.sync.dma_start(out=groups[(tag, g)][:, :, lo:hi], in_=src.rearrange("(p j) w -> p j w", j=4))

        def load_on():
            while loads:
                item = loads[0]
                if item[0] == "s":
                    c = int(item[1])
                    for mt in range(M_TILES):
                        nc.sync.dma_start(out=st_sb[mt][:, c * UNIT:(c + 1) * UNIT], in_=state[mt * P:(mt + 1) * P, c * UNIT:(c + 1) * UNIT])
                elif item == "N":
                    load_rows(noise_sb, noise_raw)
                elif item in first:
                    tag, lo, hi = first[item]
                    load_piece(0, tag, lo, hi)
                elif len(item) == 3:
                    tag, nt, c = item
                    if free_bufs[tag] == 0:
                        return
                    free_bufs[tag] -= 1
                    reads_left[item] = 2 if tag == "K" else 1
                    groups[item] = rawp.tile([P, 4, UNIT], BF16, tag=tag, name="raw%s%d%d" % (tag, nt, c), bufs=BUFS[tag])
                    src = sources[tag][c * UNIT:(c + 1) * UNIT, nt * UNIT:(nt + 1) * UNIT]
                    nc.sync.dma_start(out=groups[item][:], in_=src.rearrange("(p j) w -> p j w", j=4))
                else:
                    tag, g = item
                    if free_bufs[tag] == 0:
                        return
                    load_piece(g, tag, 0, HALF)
                loads.remove(item)

        load_on()

        def small(name, dt=F32):
            return const.tile([P, 16], dt, name=name)

        lam32 = const.tile([P, 1], F32, name="lam32")
        th = small("th")
        k_i = small("k_i", I32)
        k_f = small("k_f")
        r1 = small("r1")
        r2 = small("r2")
        a_abs = small("a_abs")
        a_ref = small("a_ref")
        a_min = small("a_min")
        z = small("z")
        ws = {k: small("w%d" % k) for k in range(1, 8)}
        tq = small("tq")
        V = nc.vector
        th_ps = psum.tile([P, P], BF16, tag="bank7", name="th_ps")
        nc.tensor.transpose(out=th_ps[:], in_=theta_rows[:], identity=ident_bf[:])
        chain = [
            lambda: V.tensor_copy(out=th[:], in_=th_ps[:, 0:16]),
            lambda: V.tensor_scalar(out=k_i[:], in0=th[:], scalar1=2.0 / math.pi, scalar2=None, op0=ALU.mult),
            lambda: V.tensor_copy(out=k_f[:], in_=k_i[:]),
            lambda: V.scalar_tensor_tensor(out=r1[:], in0=k_f[:], scalar=-HALF_PI_HI, in1=th[:], op0=ALU.mult, op1=ALU.add),
            lambda: V.scalar_tensor_tensor(out=r2[:], in0=k_f[:], scalar=-HALF_PI_LO, in1=r1[:], op0=ALU.mult, op1=ALU.add),
            lambda: V.scalar_tensor_tensor(out=a_abs[:], in0=r2[:], scalar=-1.0, in1=r2[:], op0=ALU.mult, op1=ALU.max),
            lambda: V.tensor_scalar(out=a_ref[:], in0=a_abs[:], scalar1=-1.0, scalar2=math.pi / 2, op0=ALU.mult, op1=ALU.add),
            lambda: V.tensor_tensor(out=a_min[:], in0=a_abs[:], in1=a_ref[:], op=ALU.min),
            lambda: V.tensor_tensor(out=z[:], in0=a_min[:], in1=a_min[:], op=ALU.mult),
            lambda: V.tensor_scalar(out=ws[7][:], in0=z[:], scalar1=TERMS[7], scalar2=None, op0=ALU.mult),
        ]

        def horner(k):
            return lambda: V.scalar_tensor_tensor(
                out=ws[k][:], in0=ws[k + 1][:], scalar=TERMS[k], in1=z[:], op0=ALU.add, op1=ALU.mult
            )

        for k in range(6, 0, -1):
            chain.append(horner(k))
        chain.append(
            lambda: V.scalar_tensor_tensor(out=tq[:], in0=ws[1][:], scalar=TERMS[0], in1=a_min[:], op0=ALU.add, op1=ALU.mult)
        )
        chain.append(lambda: V.tensor_copy(out=lam32[:], in_=lam_bf[:]))
        chain_pos = {"n": 0}

        def run_chain(count):
            for step in range(count):
                if chain_pos["n"] < len(chain):
                    chain[chain_pos["n"]]()
                    chain_pos["n"] += 1

        a_codes = const.tile([P, PASSES * 2 * M_ROWS], U32, name="a_codes", align_bytes=64)
        a_scales = const.tile([P, PASSES * 2 * M_ROWS], U8, name="a_scales", align_bytes=64)
        g_a = {}
        done = set()

        def spread_state(c):
            xt = psum.tile([P, 512], F32, tag="bank6", name="xt%d" % c)
            xt3 = xt[:].rearrange("p (u m) -> p u m", u=2)
            for mt in range(M_TILES):
                words = st_sb[mt][:, c * UNIT:(c + 1) * UNIT].bitcast(F32).rearrange("m (v u) -> m u v", u=2)
                for u in range(2):
                    nc.tensor.transpose(out=xt3[:, u, mt * P:(mt + 1) * P], in_=words[:, u, :], identity=ident[:])
            g_a[c] = onep.tile([P, 2048], BF16, tag="g_a", name="g_a%d" % c, align_bytes=64)
            nc.scalar.activation(
                out=g_a[c][:, 0:1024].rearrange("p (m u e) -> p m u e", u=2, e=2),
                in_=xt[:].bitcast(BF16).rearrange("p (u m e) -> p m u e", u=2, e=2),
                func=ACT.Tanh,
            )
            nc.scalar.copy(
                out=g_a[c][:, 1024:2048].bitcast(F32).rearrange("p (m u) -> p m u", u=2),
                in_=xt[:].rearrange("p (u m) -> p m u", u=2),
            )

        def quant_state(c):
            cs = slice(c * 2 * M_ROWS, (c + 1) * 2 * M_ROWS)
            nc.vector.quantize_mx(out=a_codes[:, cs].bitcast(FP8X4), scales=a_scales[:, cs], in_=g_a[c][:])
            done.add(("a", c))

        def turn(tiles, nt, bank, name):
            x = psum.tile([P, 1024], BF16, tag="bank%d" % bank, name="%s%d" % (name, nt))
            for j in range(4):
                for mt in range(M_TILES):
                    nc.tensor.transpose(
                        out=x[:, j * M_ROWS + mt * P:j * M_ROWS + (mt + 1) * P],
                        in_=tiles[mt][:, nt * UNIT + j * P:nt * UNIT + (j + 1) * P],
                        identity=ident_bf[:],
                    )
            return x

        s_t = {}

        def tanh_columns(nt):
            x = turn(st_sb, nt, 6, "sp")
            s_t[nt] = twop.tile([P, 1024], F32, tag="s_t", name="s_t%d" % nt)
            nc.scalar.activation(out=s_t[nt][:], in_=x[:], func=ACT.Tanh)

        counters = {"m": 0, "q": 0, "r": 0}
        prods = {}
        grps = {}
        codes = {}

        def mult(u):
            nt, c, mat = units[u]
            tag = "W" if mat else "J"
            prod = prodp.tile([P, 4, UNIT], BF16, tag="prod", name="prod%d" % u)
            h, k = divmod(nt, 2)
            if h in TILE_MAJOR:
                keys = {t: (t, nt, c) for t in (tag, "K")}
                views = [groups[keys[t]][:] for t in (tag, "K")]
            else:
                keys = {t: (t, h * PASSES + c) for t in (tag, "K")}
                views = [groups[keys[t]][:, :, k * UNIT:(k + 1) * UNIT] for t in (tag, "K")]
            nc.vector.tensor_tensor(out=prod[:], in0=views[0], in1=views[1], op=ALU.mult)
            prods[u] = prod
            run_chain(0 if u == 0 else 8 if u == 1 else 2)
            for t in (tag, "K"):
                reads_left[keys[t]] -= 1
                if reads_left[keys[t]] == 0:
                    free_bufs[t] += 1
            load_on()

        def regroup(u):
            grp = grpp.tile([P, 4 * UNIT], BF16, tag="grp", name="grp%d" % u, align_bytes=64)
            dst = grp[:].rearrange("p (c i t) -> p c t i", i=8, t=4)
            src = prods[u][:].rearrange("p t (c i) -> p c t i", i=8)
            if u in TENSOR_REGROUPS:
                for b in range(2):
                    px = psum.tile([P, 1024], BF16, tag="bank%d" % (4 + b), name="px%d_%d" % (u, b))
                    for t in range(4):
                        nc.tensor.matmul(
                            out=px[:].rearrange("p (n t) -> p n t", t=4)[:, :, t],
                            lhsT=ident_bf[:],
                            rhs=prods[u][:, t, b * 256:(b + 1) * 256],
                            start=True,
                            stop=True,
                        )
                    nc.scalar.copy(out=grp[:, b * 1024:(b + 1) * 1024], in_=px[:])
            elif u in VECTOR_REGROUPS:
                nc.vector.tensor_copy(out=dst, in_=src)
            else:
                nc.scalar.copy(out=dst, in_=src)
            grps[u] = grp
            counters["r"] = u + 1

        def quant(u):
            mat = "JW"[units[u][2]]
            cd = codep.tile([P, UNIT], U32, tag="codes" + mat, name="codes%d" % u, align_bytes=64)
            sc = codep.tile([P, UNIT], U8, tag="scl" + mat, name="scl%d" % u, align_bytes=64)
            nc.vector.quantize_mx(out=cd[:].bitcast(FP8X4), scales=sc[:], in_=grps[u][:])
            codes[units[u]] = (cd, sc)

        BANKS = {(nt, mat): (2, 3, 4, 5) if (nt, mat) == (3, 1) else ((0, 1), (2, 3))[nt % 2] for nt in range(4) for mat in range(2)}
        places = {}
        progress = {(nt, mat, j): 0 for nt, mat in BANKS for j in range(4)}

        def products(nt, mat):
            banks = BANKS[(nt, mat)]
            wide = len(banks) == 4
            if wide and counters["r"] <= max(TENSOR_REGROUPS + (-1,)):
                return
            if any(need not in done for need in NEEDS[(nt, mat)]):
                return
            ready = 0
            while ready < PASSES and (nt, ready, mat) in codes and ("a", ready) in done:
                ready += 1
            if ready == 0 or (not wide and ready < PASSES):
                return
            if (nt, mat) not in places:
                places[(nt, mat)] = [psum.tile([P, UNIT], F32, tag="bank%d" % b, name="ps%d_%d_%d" % (nt, mat, b)) for b in banks]
            for j in range(4):
                place = places[(nt, mat)][j if wide else j // 2]
                lo = 0 if wide else (j % 2) * M_ROWS
                for c in range(progress[(nt, mat, j)], ready):
                    cd, sc = codes[(nt, c, mat)]
                    ms = slice((2 * c + mat) * M_ROWS, (2 * c + mat + 1) * M_ROWS)
                    js = slice(j * P, (j + 1) * P)
                    nc.tensor.matmul_mx(
                        out=place[:, lo:lo + M_ROWS],
                        lhsT=cd[:, js].bitcast(FP8X4),
                        lhsT_scale=sc[:, js],
                        rhs=a_codes[:, ms].bitcast(FP8X4),
                        rhs_scale=a_scales[:, ms],
                        start=(c == 0),
                        stop=(c == PASSES - 1),
                    )
                progress[(nt, mat, j)] = ready
            if ready == PASSES:
                done.add(("mx", nt, mat))

        NEEDS = {(nt, mat): [("B", nt)] if mat else [("F", nt - 2)] if nt > 1 else [] for nt in range(4) for mat in range(2)}
        order = [(nt, mat) for h in range(2) for mat in range(2) for nt in (2 * h, 2 * h + 1)]

        def mx_catch_up():
            for key in order:
                if ("mx",) + key not in done:
                    products(*key)

        sums = {}
        nz = {}
        turned = {}

        def gain_delta(nt):
            sums[nt] = twop.tile([P, 1024], F32, tag="sum", name="sum%d" % nt)
            for b in range(2):
                bs = slice(b * UNIT, (b + 1) * UNIT)
                nc.vector.scalar_tensor_tensor(
                    out=sums[nt][:, bs], in0=places[(nt, 0)][b][:], scalar=lam32[:, 0:1], in1=s_t[nt][:, bs], op0=ALU.mult, op1=ALU.mult
                )
            done.add(("B", nt))

        def add_noise(nt):
            run_chain(len(chain))
            for j in range(4):
                js = slice(j * M_ROWS, (j + 1) * M_ROWS)
                nc.vector.scalar_tensor_tensor(
                    out=sums[nt][:, js], in0=nz[nt][:, js], scalar=tq[:, 4 * nt + j:4 * nt + j + 1], in1=sums[nt][:, js], op0=ALU.mult, op1=ALU.add
                )
            done.add(("A", nt))

        def add_signal(nt):
            pl = places[(nt, 1)]
            n = 1024 // len(pl)
            for b in range(len(pl)):
                bs = slice(b * n, (b + 1) * n)
                nc.vector.tensor_tensor(out=sums[nt][:, bs], in0=pl[b][:, 0:n], in1=sums[nt][:, bs], op=ALU.add)
            done.add(("D", nt))

        def turn_back(nt):
            for mt in range(M_TILES):
                o = psum.tile([P, UNIT], F32, tag="bank%d" % BANKS[(nt, 1)][mt], name="o%d%d" % (nt, mt))
                for j in range(4):
                    nc.tensor.transpose(out=o[:, j * P:(j + 1) * P], in_=sums[nt][:, j * M_ROWS + mt * P:j * M_ROWS + (mt + 1) * P], identity=ident[:])
                turned[(nt, mt)] = o

        def finish(nt):
            for mt in range(M_TILES):
                y = outp.tile([P, UNIT], F32, tag="y", name="y%d%d" % (nt, mt))
                nc.scalar.activation(out=y[:], in_=turned[(nt, mt)][:], func=ACT.Tanh)
                nc.sync.dma_start(out=out[mt * P:(mt + 1) * P, nt * UNIT:(nt + 1) * UNIT], in_=y[:])
            done.add(("F", nt))

        def finish_last(nt):
            ys = [outp.tile([P, UNIT], F32, tag="y", name="y%d%d" % (nt, mt)) for mt in range(M_TILES)]
            for half in range(2):
                obanks = [psum.tile([P, UNIT], F32, tag="bank%d" % ((0, 1, 6, 7)[2 * half + mt]), name="o%d%d%d" % (nt, mt, half)) for mt in range(M_TILES)]
                for jj in range(2):
                    j = 2 * half + jj
                    for mt in range(M_TILES):
                        nc.tensor.transpose(out=obanks[mt][:, jj * P:(jj + 1) * P], in_=sums[nt][:, j * M_ROWS + mt * P:j * M_ROWS + (mt + 1) * P], identity=ident[:])
                for mt in range(M_TILES):
                    hs = slice(half * M_ROWS, (half + 1) * M_ROWS)
                    nc.scalar.activation(out=ys[mt][:, hs], in_=obanks[mt][:, 0:M_ROWS], func=ACT.Tanh)
                    col = nt * UNIT + half * M_ROWS
                    nc.sync.dma_start(out=out[mt * P:(mt + 1) * P, col:col + M_ROWS], in_=ys[mt][:, hs])

        run_chain(CHAIN_FIRST)

        def mults_to(lim):
            while counters["m"] <= min(lim, UNITS - 1):
                mult(counters["m"])
                counters["m"] += 1

        def quants_to(lim):
            while counters["q"] <= min(lim, UNITS - 1):
                quant(counters["q"])
                counters["q"] += 1
                mx_catch_up()

        stage = {nt: (0, 0) for nt in range(4)}
        for i in range(UNITS + 12):
            if i < UNITS:
                mults_to(i)
                regroup(i)
            for q in range(PASSES):
                if i == ST0 + STD * q:
                    spread_state(q)
            for nt in range(4):
                if i == last[(nt, 0)] - S_BEFORE:
                    tanh_columns(nt)
            quants_to(i - QLAG)
            for q in range(PASSES):
                if i == ST0 + STD * q + STQ:
                    quant_state(q)
            mx_catch_up()
            for nt in range(4):
                step, at = stage[nt]
                if step == 0 and ("mx", nt, 0) in done and (nt == 0 or ("A", nt - 1) in done) and i >= last[(nt, 0)] + QLAG + B_LAG:
                    gain_delta(nt)
                    nz[nt] = turn(noise_sb, nt, 7, "nz")
                    stage[nt] = (1, i)
                elif step == 1 and i >= at + (A_LAG if nt < 3 else A_LAST):
                    add_noise(nt)
                    stage[nt] = (2, i)
                elif step == 2 and ("mx", nt, 1) in done and i >= last[(nt, 1)] + QLAG + (0 if last[(nt, 1)] >= UNITS - 2 else D_LAG):
                    add_signal(nt)
                    stage[nt] = (3, i)
                    if nt == 3:
                        finish_last(nt)
                    elif nt == 2 and 1 not in TILE_MAJOR:
                        turn_back(nt)
                        finish(nt)
                        stage[nt] = (5, i)
                elif step == 3 and i >= at + O_LAG and nt < 3:
                    turn_back(nt)
                    stage[nt] = (4, i)
                elif step == 4 and i >= at + F_LAG:
                    finish(nt)
                    stage[nt] = (5, i)
            mults_to(i + lead(i))
            mx_catch_up()
